import numpy as np
import ml_dtypes


def mxq(x, axis, fmt="e4m3"):
    dtype, down = {"e4m3": (ml_dtypes.float8_e4m3fn, 7), "e5m2": (ml_dtypes.float8_e5m2, 14)}[fmt]
    v = np.moveaxis(np.asarray(x, np.float32).astype(ml_dtypes.bfloat16).astype(np.float64), axis, -1)
    blocks = v.reshape(v.shape[:-1] + (-1, 32))
    amax = np.abs(blocks).max(-1, keepdims=True)
    byte = np.maximum(np.where(amax > 0, np.frexp(amax)[1] - 1 + 127, 0) - down, 1)
    scale = np.exp2(byte - 127.0)
    codes = (blocks / scale).astype(np.float32).astype(dtype).astype(np.float64)
    return np.moveaxis((codes * scale).reshape(v.shape), -1, axis)


WIDE = False


def mx_kscale(k):
    if not WIDE:
        return np.ones(k)
    levels = np.array([10, -10, 5, -5, 0])
    a = np.random.permutation(np.resize(levels, k // 512 * 4)).reshape(k // 512, 4)
    idx = np.arange(k)
    return np.exp2(a[idx // 512, idx % 128 // 32])


BF16 = ml_dtypes.bfloat16


def bf(x):
    return np.asarray(x, np.float32).astype(BF16)


def f64(x):
    return np.asarray(x).astype(np.float64)


E2M1 = np.array([0.0, 0.5, 1.0, 1.5, 2.0, 3.0, 4.0, 6.0, -0.0, -0.5, -1.0, -1.5, -2.0, -3.0, -4.0, -6.0])


def pack_weight(w, fmt):
    k, n = w.shape
    w = f64(bf(w)).reshape(k // 32, 32, n)
    amax = np.abs(w).max(1)
    if fmt == "e4m3":
        byte = np.frexp(amax)[1] - 1 + 127 - 7
    else:
        mant, ex = np.frexp(amax / 6.0)
        byte = np.where(mant > 0.5, ex, ex - 1) + 127
    byte = np.clip(np.where(amax > 0, byte, 1), 1, 254)
    scaled = (w * np.exp2(127.0 - byte)[:, None, :]).reshape(k, n).astype(np.float32)
    by_word = np.ascontiguousarray(scaled.reshape(k // 512, 128, 4, n).transpose(0, 1, 3, 2))
    if fmt == "e4m3":
        words = by_word.astype(ml_dtypes.float8_e4m3fn).view(np.uint8)
    else:
        c = by_word.astype(ml_dtypes.float4_e2m1fn).view(np.uint8) & 0xF
        words = c[..., 0::2] | (c[..., 1::2] << 4)
    return np.ascontiguousarray(words), np.ascontiguousarray(byte.astype(np.uint8).reshape(k // 512, 16, n))


def unpack_weight(words, scales, fmt):
    g, p, n, _ = words.shape
    if fmt == "e4m3":
        vals = np.ascontiguousarray(words).view(ml_dtypes.float8_e4m3fn).astype(np.float64)
    else:
        nib = np.empty((g, p, n, 4), np.uint8)
        nib[..., 0::2] = words & 0xF
        nib[..., 1::2] = words >> 4
        vals = E2M1[nib]
    vals = vals * np.repeat(np.exp2(scales.astype(np.float64) - 127.0), 8, axis=1)[..., None]
    return vals.transpose(0, 1, 3, 2).reshape(g * 512, n)


BATCH, ROWS, COLS, IN_DIM, OUT_DIM = 2, 8, 8, 4096, 4096
N = ROWS * COLS
EPS_BN = 1e-5
EPS_DEG = 1e-5
FMT = "e4m3"


def _stencil9(x):
    R, C = x.shape[-3], x.shape[-2]
    pad = [(0, 0)] * (x.ndim - 3) + [(1, 1), (1, 1), (0, 0)]
    xp = np.pad(x, pad)
    out = np.zeros_like(x)
    for di in range(3):
        for dj in range(3):
            out = out + xp[..., di:di + R, dj:dj + C, :]
    return out


def _deg_inv_sqrt(rows, cols):
    D = _stencil9(np.ones((rows, cols, 1)))[..., 0]
    return (D + EPS_DEG) ** -0.5


def setup_inputs():
    s = mx_kscale(IN_DIM)
    mu = 0.5 * np.random.standard_normal(IN_DIM)
    bound = np.sqrt(6.0 / IN_DIM)
    H = bf((np.random.standard_normal((BATCH, N, IN_DIM)) + mu) * s)
    W_words, W_scales = pack_weight(np.random.uniform(-bound, bound, (IN_DIM, OUT_DIM)) / s[:, None], FMT)
    return {"H": H,
            "W_words": W_words,
            "W_scales": W_scales,
            "gamma": bf(1.0 + 0.1 * np.random.standard_normal(OUT_DIM)),
            "beta": bf(0.2 * np.random.standard_normal(OUT_DIM))}


def reference(H, W_words, W_scales, gamma, beta):
    B, n_nodes, _ = H.shape
    Ht = mxq(f64(H), 2, "e4m3") @ unpack_weight(W_words, W_scales, FMT)
    mean = Ht.mean(axis=(0, 1))
    var = Ht.var(axis=(0, 1))
    Ht = (Ht - mean) * (1.0 / np.sqrt(var + EPS_BN)) * f64(gamma) + f64(beta)
    Ht = np.maximum(Ht, 0.0)
    d = _deg_inv_sqrt(ROWS, COLS)[None, :, :, None]
    Hg = Ht.reshape(B, ROWS, COLS, OUT_DIM)
    Hagg = d * _stencil9(Hg * d)
    return Hagg.reshape(B, n_nodes, OUT_DIM)

@@ -1,0 +1,203 @@
+from contextlib import ExitStack
+
+import concourse.mybir as mybir
+from concourse.masks import make_identity
+
+F32 = mybir.dt.float32
+BF16 = mybir.dt.bfloat16
+I32 = mybir.dt.int32
+U32 = mybir.dt.uint32
+U8 = mybir.dt.uint8
+FP8X4 = mybir.dt.float8_e4m3fn_x4
+ACT = mybir.ActivationFunctionType
+
+P = 128
+BATCH, GRID = 2, 8
+K = 4096
+FEATURES = 4096
+PACK = 4
+K_PASS = P * PACK
+PASSES = K // K_PASS
+PLANES_PER_TILE = 4
+TILE_F = P
+BLOCK_TILES = 4
+BLOCK_F = BLOCK_TILES * TILE_F
+BLOCKS = FEATURES // BLOCK_F
+EPS_BN = 1e-5
+EPS_DEG = 1e-5
+
+FLOPS = 2 * P * K * FEATURES
+
+
+def tile_graphconvolutionbatch_w_kernel(tc, H, W_words, W_scales, gamma, beta, out):
+    nc = tc.nc
+    h_rows = H.rearrange("b n k -> (b n) k")
+    out_rows = out.rearrange("b n f -> (b n) f")
+    w_words = W_words.rearrange("g p n t -> g p (n t)").bitcast(I32).rearrange("g p n -> p g n")
+    w_scale_rows = W_scales.bitcast(I32)
+
+    with ExitStack() as ctx:
+        consts = ctx.enter_context(tc.tile_pool(name="consts", bufs=1))
+        weights = ctx.enter_context(tc.tile_pool(name="weights", bufs=1))
+        small = ctx.enter_context(tc.tile_pool(name="small", bufs=4))
+        work = ctx.enter_context(tc.tile_pool(name="work", bufs=3))
+
+        w_planes = consts.tile([P, PASSES // PLANES_PER_TILE, FEATURES], U8, align_bytes=64)
+        nc.vector.memset(w_planes[:].bitcast(I32), 0)
+
+        h_sb = consts.tile([P, K], BF16)
+        for pair in range(PASSES // 2):
+            cols = slice(2 * K_PASS * pair, 2 * K_PASS * (pair + 1))
+            nc.sync.dma_start(out=h_sb[:, cols], in_=h_rows[:, cols])
+
+        for half in range(PASSES // PLANES_PER_TILE):
+            for quad in range(4):
+                nc.sync.dma_start(
+                    out=w_planes[32 * quad : 32 * quad + 16, half, :].bitcast(I32),
+                    in_=w_scale_rows[4 * half : 4 * half + 4, 4 * quad : 4 * quad + 4, :],
+                )
+
+        w_codes = []
+        for n in range(BLOCKS):
+            block_codes = weights.tile([P, PASSES, BLOCK_F], U32, name="w_codes_%d" % n, align_bytes=64)
+            nc.sync.dma_start(
+                out=block_codes[:].bitcast(I32), in_=w_words[:, :, BLOCK_F * n : BLOCK_F * (n + 1)]
+            )
+            w_codes.append(block_codes)
+
+        gb_rows = consts.tile([P, TILE_F], BF16)
+        nc.vector.memset(gb_rows[:], 0.0)
+        n_tiles = FEATURES // TILE_F
+        nc.scalar.dma_start(out=gb_rows[0:n_tiles, :], in_=gamma.rearrange("(t f) -> t f", f=TILE_F))
+        nc.scalar.dma_start(out=gb_rows[n_tiles : 2 * n_tiles, :], in_=beta.rearrange("(t f) -> t f", f=TILE_F))
+
+        ident = consts.tile([P, P], F32)
+        make_identity(nc, ident[:])
+        eps_bn = consts.tile([P, 1], F32)
+        nc.vector.memset(eps_bn[:], EPS_BN)
+        eps_deg = consts.tile([P, 1], F32)
+        nc.vector.memset(eps_deg[:], EPS_DEG)
+
+        ident_c = ident[:].rearrange("p (s c) -> p s c", c=GRID)
+        along_c = consts.tile([P, BATCH * GRID, GRID], F32)
+        nc.vector.tensor_copy(out=along_c[:], in_=ident_c)
+        nc.vector.tensor_add(out=along_c[:, :, 1:GRID], in0=along_c[:, :, 1:GRID], in1=ident_c[:, :, 0 : GRID - 1])
+        nc.vector.tensor_add(out=along_c[:, :, 0 : GRID - 1], in0=along_c[:, :, 0 : GRID - 1], in1=ident_c[:, :, 1:GRID])
+        along_c_r = along_c[:].rearrange("p (b r) c -> p b (r c)", b=BATCH)
+        neighbours = consts.tile([P, BATCH, GRID * GRID], F32)
+        nc.vector.tensor_copy(out=neighbours[:], in_=along_c_r)
+        inner = GRID * (GRID - 1)
+        nc.vector.tensor_add(out=neighbours[:, :, GRID:], in0=neighbours[:, :, GRID:], in1=along_c_r[:, :, 0:inner])
+        nc.vector.tensor_add(out=neighbours[:, :, 0:inner], in0=neighbours[:, :, 0:inner], in1=along_c_r[:, :, GRID:])
+        neighbours_2d = neighbours[:].rearrange("p b s -> p (b s)")
+
+        degree = consts.tile([P, 1], F32)
+        nc.vector.reduce_sum(out=degree[:], in_=neighbours_2d, axis=mybir.AxisListType.X)
+        d_sqrt = consts.tile([P, 1], F32)
+        nc.scalar.activation(out=d_sqrt[:], in_=degree[:], func=ACT.Sqrt, bias=eps_deg[:, 0:1])
+        d = consts.tile([P, 1], F32)
+        nc.vector.reciprocal(out=d[:], in_=d_sqrt[:])
+        neighbours_d = consts.tile([P, P], F32)
+        nc.vector.tensor_scalar_mul(out=neighbours_d[:], in0=neighbours_2d, scalar1=d[:, 0:1])
+
+        grouped = consts.tile([P, PASSES, P, PACK], BF16, align_bytes=64)
+        h_codes = consts.tile([P, PASSES, P], U32, align_bytes=64)
+        h_scales = consts.tile([P, PASSES, P], U8, align_bytes=64)
+        gb = consts.tile([P, 2 * n_tiles], F32)
+        with tc.psum_pool(name="head_psum", bufs=1) as head_psum:
+            h_pairs = h_sb[:].bitcast(F32)
+            grouped_pairs = grouped[:].bitcast(F32)
+            for pair in range(PASSES // 2):
+                flipped = head_psum.tile([P, 2, 2, P], F32, name="flipped_%d" % pair)
+                for gg in range(2):
+                    g = 2 * pair + gg
+                    for u in range(2):
+                        nc.tensor.transpose(
+                            flipped[:, gg, u, :], h_pairs[:, 256 * g + u : 256 * (g + 1) : 2], ident[:]
+                        )
+                dst = grouped_pairs[:, 2 * pair : 2 * pair + 2, :, :]
+                src = flipped[:].rearrange("p g u r -> p g r u")
+                if pair % 2 == 0:
+                    nc.vector.tensor_copy(out=dst, in_=src)
+                else:
+                    nc.scalar.copy(out=dst, in_=src)
+            for pair in range(PASSES // 2):
+                gs = slice(2 * pair, 2 * pair + 2)
+                nc.vector.quantize_mx(
+                    out=h_codes[:, gs, :].rearrange("p g r -> p (g r)").bitcast(FP8X4),
+                    scales=h_scales[:, gs, :].rearrange("p g r -> p (g r)"),
+                    in_=grouped[:, gs, :, :].rearrange("p g r t -> p (g r t)"),
+                )
+
+            gb_rows_f32 = consts.tile([P, TILE_F], F32)
+            nc.vector.tensor_copy(out=gb_rows_f32[:], in_=gb_rows[:])
+            gb_flipped = head_psum.tile([P, P], F32)
+            nc.tensor.transpose(gb_flipped[:], gb_rows_f32[:], ident[:])
+            nc.vector.tensor_copy(out=gb[:], in_=gb_flipped[:, 0 : 2 * n_tiles])
+
+        acc_psum = ctx.enter_context(tc.psum_pool(name="acc_psum", bufs=3))
+        flip_psum = ctx.enter_context(tc.psum_pool(name="flip_psum", bufs=2))
+        agg_psum = ctx.enter_context(tc.psum_pool(name="agg_psum", bufs=2))
+
+        def multiply_and_normalise(n):
+            acc = acc_psum.tile([P, BLOCK_TILES, P], F32)
+            for i in range(BLOCK_TILES):
+                f_cols = slice(TILE_F * i, TILE_F * (i + 1))
+                plane_cols = slice(BLOCK_F * n + TILE_F * i, BLOCK_F * n + TILE_F * (i + 1))
+                for g in range(PASSES):
+                    offset = 4 * (g % PLANES_PER_TILE)
+                    nc.tensor.matmul_mx(
+                        out=acc[:, i, :],
+                        lhsT=w_codes[n][:, g, f_cols].bitcast(FP8X4),
+                        lhsT_scale=w_planes[offset:P, g // PLANES_PER_TILE, plane_cols],
+                        rhs=h_codes[:, g, :].bitcast(FP8X4),
+                        rhs_scale=h_scales[:, g, :],
+                        start=(g == 0),
+                        stop=(g == PASSES - 1),
+                    )
+            stats = small.tile([P, BLOCK_TILES, 6], F32)
+            mean_var = small.tile([P, BLOCK_TILES, 2], F32)
+            for i in range(BLOCK_TILES):
+                nc.vector.bn_stats(out=stats[:, i, :], in_=acc[:, i, :])
+                nc.vector.bn_aggr(out=mean_var[:, i, :], in_=stats[:, i, :])
+            std = small.tile([P, BLOCK_TILES], F32)
+            nc.scalar.activation(out=std[:], in_=mean_var[:, :, 1], func=ACT.Sqrt, bias=eps_bn[:, 0:1])
+            gain = small.tile([P, BLOCK_TILES], F32)
+            nc.vector.reciprocal(out=gain[:], in_=std[:])
+            tiles = slice(BLOCK_TILES * n, BLOCK_TILES * (n + 1))
+            nc.vector.tensor_mul(out=gain[:], in0=gain[:], in1=gb[:, tiles])
+            shift = small.tile([P, BLOCK_TILES], F32)
+            nc.vector.tensor_mul(out=shift[:], in0=mean_var[:, :, 0], in1=gain[:])
+            beta_cols = slice(n_tiles + BLOCK_TILES * n, n_tiles + BLOCK_TILES * (n + 1))
+            nc.vector.tensor_sub(out=shift[:], in0=gb[:, beta_cols], in1=shift[:])
+            z = work.tile([P, BLOCK_TILES, P], F32)
+            for i in range(BLOCK_TILES):
+                nc.scalar.activation(
+                    out=z[:, i, :], in_=acc[:, i, :], func=ACT.Relu, bias=shift[:, i : i + 1], scale=gain[:, i : i + 1]
+                )
+            return z
+
+        def flip(z):
+            z_flipped = flip_psum.tile([P, BLOCK_F], F32)
+            for i in range(BLOCK_TILES):
+                nc.tensor.transpose(z_flipped[:, TILE_F * i : TILE_F * (i + 1)], z[:, i, :], ident[:])
+            z_rows = work.tile([P, BLOCK_F], F32)
+            nc.vector.tensor_copy(out=z_rows[:], in_=z_flipped[:])
+            return z_rows
+
+        def aggregate_and_store(n, z_rows):
+            summed = agg_psum.tile([P, BLOCK_F], F32)
+            nc.tensor.matmul(out=summed[:], lhsT=neighbours_d[:], rhs=z_rows[:], start=True, stop=True)
+            result = work.tile([P, BLOCK_F], F32)
+            nc.scalar.activation(out=result[:], in_=summed[:], func=ACT.Copy, scale=d[:, 0:1])
+            nc.scalar.dma_start(out=out_rows[:, BLOCK_F * n : BLOCK_F * (n + 1)], in_=result[:])
+
+        z_tiles = {}
+        z_rows_tiles = {}
+        for n in range(BLOCKS + 2):
+            if n < BLOCKS:
+                z_tiles[n] = multiply_and_normalise(n)
+            if 1 <= n <= BLOCKS:
+                z_rows_tiles[n - 1] = flip(z_tiles[n - 1])
+            if n >= 2:
+                aggregate_and_store(n - 2, z_rows_tiles[n - 2])

@@ -10,6 +10,7 @@ U32 = mybir.dt.uint32
 U8 = mybir.dt.uint8
 FP8X4 = mybir.dt.float8_e4m3fn_x4
 ACT = mybir.ActivationFunctionType
+ALU = mybir.AluOpType
 
 P = 128
 BATCH, GRID = 2, 8
@@ -19,10 +20,12 @@ PACK = 4
 K_PASS = P * PACK
 PASSES = K // K_PASS
 PLANES_PER_TILE = 4
-TILE_F = P
-BLOCK_TILES = 4
-BLOCK_F = BLOCK_TILES * TILE_F
-BLOCKS = FEATURES // BLOCK_F
+BANK_F = 512
+TILES_PER_BANK = BANK_F // P
+RANGE_BANKS = 2
+RANGE_F = RANGE_BANKS * BANK_F
+RANGES = FEATURES // RANGE_F
+N_TILES = FEATURES // P
 EPS_BN = 1e-5
 EPS_DEG = 1e-5
 
@@ -58,18 +61,18 @@ def tile_graphconvolutionbatch_w_kernel(tc, H, W_words, W_scales, gamma, beta, o
                 )
 
         w_codes = []
-        for n in range(BLOCKS):
-            block_codes = weights.tile([P, PASSES, BLOCK_F], U32, name="w_codes_%d" % n, align_bytes=64)
-            nc.sync.dma_start(
-                out=block_codes[:].bitcast(I32), in_=w_words[:, :, BLOCK_F * n : BLOCK_F * (n + 1)]
-            )
-            w_codes.append(block_codes)
+        for r in range(RANGES):
+            range_codes = weights.tile([P, PASSES, RANGE_F], U32, name="w_codes_%d" % r, align_bytes=64)
+            for g in range(PASSES):
+                nc.sync.dma_start(
+                    out=range_codes[:, g, :].bitcast(I32), in_=w_words[:, g, RANGE_F * r : RANGE_F * (r + 1)]
+                )
+            w_codes.append(range_codes)
 
-        gb_rows = consts.tile([P, TILE_F], BF16)
+        gb_rows = consts.tile([P, P], BF16)
         nc.vector.memset(gb_rows[:], 0.0)
-        n_tiles = FEATURES // TILE_F
-        nc.scalar.dma_start(out=gb_rows[0:n_tiles, :], in_=gamma.rearrange("(t f) -> t f", f=TILE_F))
-        nc.scalar.dma_start(out=gb_rows[n_tiles : 2 * n_tiles, :], in_=beta.rearrange("(t f) -> t f", f=TILE_F))
+        nc.scalar.dma_start(out=gb_rows[0:N_TILES, :], in_=gamma.rearrange("(t f) -> t f", f=P))
+        nc.scalar.dma_start(out=gb_rows[N_TILES : 2 * N_TILES, :], in_=beta.rearrange("(t f) -> t f", f=P))
 
         ident = consts.tile([P, P], F32)
         make_identity(nc, ident[:])
@@ -97,13 +100,14 @@ def tile_graphconvolutionbatch_w_kernel(tc, H, W_words, W_scales, gamma, beta, o
         nc.scalar.activation(out=d_sqrt[:], in_=degree[:], func=ACT.Sqrt, bias=eps_deg[:, 0:1])
         d = consts.tile([P, 1], F32)
         nc.vector.reciprocal(out=d[:], in_=d_sqrt[:])
-        neighbours_d = consts.tile([P, P], F32)
-        nc.vector.tensor_scalar_mul(out=neighbours_d[:], in0=neighbours_2d, scalar1=d[:, 0:1])
+        scaled_once = consts.tile([P, P], F32)
+        nc.vector.tensor_scalar_mul(out=scaled_once[:], in0=neighbours_2d, scalar1=d[:, 0:1])
 
         grouped = consts.tile([P, PASSES, P, PACK], BF16, align_bytes=64)
         h_codes = consts.tile([P, PASSES, P], U32, align_bytes=64)
         h_scales = consts.tile([P, PASSES, P], U8, align_bytes=64)
-        gb = consts.tile([P, 2 * n_tiles], F32)
+        gb = consts.tile([P, 2 * N_TILES], F32)
+        aggregation = consts.tile([P, P], F32)
         with tc.psum_pool(name="head_psum", bufs=1) as head_psum:
             h_pairs = h_sb[:].bitcast(F32)
             grouped_pairs = grouped[:].bitcast(F32)
@@ -129,75 +133,83 @@ def tile_graphconvolutionbatch_w_kernel(tc, H, W_words, W_scales, gamma, beta, o
                     in_=grouped[:, gs, :, :].rearrange("p g r t -> p (g r t)"),
                 )
 
-            gb_rows_f32 = consts.tile([P, TILE_F], F32)
+            gb_rows_f32 = consts.tile([P, P], F32)
             nc.vector.tensor_copy(out=gb_rows_f32[:], in_=gb_rows[:])
             gb_flipped = head_psum.tile([P, P], F32)
             nc.tensor.transpose(gb_flipped[:], gb_rows_f32[:], ident[:])
-            nc.vector.tensor_copy(out=gb[:], in_=gb_flipped[:, 0 : 2 * n_tiles])
+            nc.vector.tensor_copy(out=gb[:], in_=gb_flipped[:, 0 : 2 * N_TILES])
 
-        acc_psum = ctx.enter_context(tc.psum_pool(name="acc_psum", bufs=3))
-        flip_psum = ctx.enter_context(tc.psum_pool(name="flip_psum", bufs=2))
+            scaled_flipped = head_psum.tile([P, P], F32)
+            nc.tensor.transpose(scaled_flipped[:], scaled_once[:], ident[:])
+            nc.vector.tensor_scalar_mul(out=aggregation[:], in0=scaled_flipped[:], scalar1=d[:, 0:1])
+
+        acc_psum = ctx.enter_context(tc.psum_pool(name="acc_psum", bufs=2 * RANGE_BANKS))
+        flip_psum = ctx.enter_context(tc.psum_pool(name="flip_psum", bufs=1))
         agg_psum = ctx.enter_context(tc.psum_pool(name="agg_psum", bufs=2))
 
-        def multiply_and_normalise(n):
-            acc = acc_psum.tile([P, BLOCK_TILES, P], F32)
-            for i in range(BLOCK_TILES):
-                f_cols = slice(TILE_F * i, TILE_F * (i + 1))
-                plane_cols = slice(BLOCK_F * n + TILE_F * i, BLOCK_F * n + TILE_F * (i + 1))
-                for g in range(PASSES):
-                    offset = 4 * (g % PLANES_PER_TILE)
+        def multiply(r):
+            sums = [acc_psum.tile([P, BANK_F], F32, name="acc") for b in range(RANGE_BANKS)]
+            for g in range(PASSES):
+                offset = 4 * (g % PLANES_PER_TILE)
+                for b in range(RANGE_BANKS):
+                    first = RANGE_F * r + BANK_F * b
                     nc.tensor.matmul_mx(
-                        out=acc[:, i, :],
-                        lhsT=w_codes[n][:, g, f_cols].bitcast(FP8X4),
-                        lhsT_scale=w_planes[offset:P, g // PLANES_PER_TILE, plane_cols],
-                        rhs=h_codes[:, g, :].bitcast(FP8X4),
-                        rhs_scale=h_scales[:, g, :],
+                        out=sums[b][:],
+                        lhsT=h_codes[:, g, :].bitcast(FP8X4),
+                        lhsT_scale=h_scales[:, g, :],
+                        rhs=w_codes[r][:, g, BANK_F * b : BANK_F * (b + 1)].bitcast(FP8X4),
+                        rhs_scale=w_planes[offset:P, g // PLANES_PER_TILE, first : first + BANK_F],
                         start=(g == 0),
                         stop=(g == PASSES - 1),
                     )
-            stats = small.tile([P, BLOCK_TILES, 6], F32)
-            mean_var = small.tile([P, BLOCK_TILES, 2], F32)
-            for i in range(BLOCK_TILES):
-                nc.vector.bn_stats(out=stats[:, i, :], in_=acc[:, i, :])
+            return sums
+
+        def finish(bank, acc):
+            y_rows = work.tile([P, BANK_F], F32)
+            nc.scalar.copy(out=y_rows[:], in_=acc[:])
+            y_feat = flip_psum.tile([P, TILES_PER_BANK, P], F32)
+            for i in range(TILES_PER_BANK):
+                nc.tensor.transpose(y_feat[:, i, :], y_rows[:, P * i : P * (i + 1)], ident[:])
+
+            stats = small.tile([P, TILES_PER_BANK, 6], F32)
+            mean_var = small.tile([P, TILES_PER_BANK, 2], F32)
+            for i in range(TILES_PER_BANK):
+                nc.vector.bn_stats(out=stats[:, i, :], in_=y_feat[:, i, :])
                 nc.vector.bn_aggr(out=mean_var[:, i, :], in_=stats[:, i, :])
-            std = small.tile([P, BLOCK_TILES], F32)
+            std = small.tile([P, TILES_PER_BANK], F32)
             nc.scalar.activation(out=std[:], in_=mean_var[:, :, 1], func=ACT.Sqrt, bias=eps_bn[:, 0:1])
-            gain = small.tile([P, BLOCK_TILES], F32)
+            gain = small.tile([P, TILES_PER_BANK], F32)
             nc.vector.reciprocal(out=gain[:], in_=std[:])
-            tiles = slice(BLOCK_TILES * n, BLOCK_TILES * (n + 1))
-            nc.vector.tensor_mul(out=gain[:], in0=gain[:], in1=gb[:, tiles])
-            shift = small.tile([P, BLOCK_TILES], F32)
+            first_tile = TILES_PER_BANK * bank
+            nc.vector.tensor_mul(out=gain[:], in0=gain[:], in1=gb[:, first_tile : first_tile + TILES_PER_BANK])
+            shift = small.tile([P, TILES_PER_BANK], F32)
             nc.vector.tensor_mul(out=shift[:], in0=mean_var[:, :, 0], in1=gain[:])
-            beta_cols = slice(n_tiles + BLOCK_TILES * n, n_tiles + BLOCK_TILES * (n + 1))
-            nc.vector.tensor_sub(out=shift[:], in0=gb[:, beta_cols], in1=shift[:])
-            z = work.tile([P, BLOCK_TILES, P], F32)
-            for i in range(BLOCK_TILES):
-                nc.scalar.activation(
-                    out=z[:, i, :], in_=acc[:, i, :], func=ACT.Relu, bias=shift[:, i : i + 1], scale=gain[:, i : i + 1]
+            first_beta = N_TILES + first_tile
+            nc.vector.tensor_sub(out=shift[:], in0=gb[:, first_beta : first_beta + TILES_PER_BANK], in1=shift[:])
+            normed = work.tile([P, TILES_PER_BANK, P], F32)
+            for i in range(TILES_PER_BANK):
+                nc.vector.tensor_scalar(
+                    out=normed[:, i, :],
+                    in0=y_feat[:, i, :],
+                    scalar1=gain[:, i : i + 1],
+                    scalar2=shift[:, i : i + 1],
+                    op0=ALU.mult,
+                    op1=ALU.add,
                 )
-            return z
 
-        def flip(z):
-            z_flipped = flip_psum.tile([P, BLOCK_F], F32)
-            for i in range(BLOCK_TILES):
-                nc.tensor.transpose(z_flipped[:, TILE_F * i : TILE_F * (i + 1)], z[:, i, :], ident[:])
-            z_rows = work.tile([P, BLOCK_F], F32)
-            nc.vector.tensor_copy(out=z_rows[:], in_=z_flipped[:])
-            return z_rows
+            normed_rows = flip_psum.tile([P, BANK_F], F32)
+            for i in range(TILES_PER_BANK):
+                nc.tensor.transpose(normed_rows[:, P * i : P * (i + 1)], normed[:, i, :], ident[:])
+            z_rows = work.tile([P, BANK_F], F32)
+            nc.scalar.activation(out=z_rows[:], in_=normed_rows[:], func=ACT.Relu)
 
-        def aggregate_and_store(n, z_rows):
-            summed = agg_psum.tile([P, BLOCK_F], F32)
-            nc.tensor.matmul(out=summed[:], lhsT=neighbours_d[:], rhs=z_rows[:], start=True, stop=True)
-            result = work.tile([P, BLOCK_F], F32)
-            nc.scalar.activation(out=result[:], in_=summed[:], func=ACT.Copy, scale=d[:, 0:1])
-            nc.scalar.dma_start(out=out_rows[:, BLOCK_F * n : BLOCK_F * (n + 1)], in_=result[:])
+            summed = agg_psum.tile([P, BANK_F], F32)
+            nc.tensor.matmul(out=summed[:], lhsT=aggregation[:], rhs=z_rows[:], start=True, stop=True)
+            result = work.tile([P, BANK_F], F32)
+            nc.scalar.copy(out=result[:], in_=summed[:])
+            nc.scalar.dma_start(out=out_rows[:, BANK_F * bank : BANK_F * (bank + 1)], in_=result[:])
 
-        z_tiles = {}
-        z_rows_tiles = {}
-        for n in range(BLOCKS + 2):
-            if n < BLOCKS:
-                z_tiles[n] = multiply_and_normalise(n)
-            if 1 <= n <= BLOCKS:
-                z_rows_tiles[n - 1] = flip(z_tiles[n - 1])
-            if n >= 2:
-                aggregate_and_store(n - 2, z_rows_tiles[n - 2])
+        for r in range(RANGES):
+            sums = multiply(r)
+            for b in range(RANGE_BANKS):
+                finish(RANGE_BANKS * r + b, sums[b])

@@ -21,15 +21,25 @@ K_PASS = P * PACK
 PASSES = K // K_PASS
 PLANES_PER_TILE = 4
 BANK_F = 512
-TILES_PER_BANK = BANK_F // P
-RANGE_BANKS = 2
-RANGE_F = RANGE_BANKS * BANK_F
-RANGES = FEATURES // RANGE_F
+FIRST_F = 512
+LAST_F = 256
+PIECE_WORDS = 1024
+EARLY_PASSES = 2
 N_TILES = FEATURES // P
 EPS_BN = 1e-5
 EPS_DEG = 1e-5
 
 FLOPS = 2 * P * K * FEATURES
+
+
+def halvings(total, smallest):
+    widths = []
+    left = total
+    while left > smallest:
+        left //= 2
+        widths.append(left)
+    widths.append(left)
+    return widths
 
 
 def tile_graphconvolutionbatch_w_kernel(tc, H, W_words, W_scales, gamma, beta, out):
@@ -39,35 +49,54 @@ def tile_graphconvolutionbatch_w_kernel(tc, H, W_words, W_scales, gamma, beta, o
     w_words = W_words.rearrange("g p n t -> g p (n t)").bitcast(I32).rearrange("g p n -> p g n")
     w_scale_rows = W_scales.bitcast(I32)
 
+    half_f = FEATURES // 2
+    range_widths = list(reversed(halvings(half_f, FIRST_F))) + halvings(half_f, LAST_F)
+
     with ExitStack() as ctx:
+        ctx.enter_context(tc.manual_schedule())
         consts = ctx.enter_context(tc.tile_pool(name="consts", bufs=1))
         weights = ctx.enter_context(tc.tile_pool(name="weights", bufs=1))
+        results = ctx.enter_context(tc.tile_pool(name="results", bufs=1))
         small = ctx.enter_context(tc.tile_pool(name="small", bufs=4))
         work = ctx.enter_context(tc.tile_pool(name="work", bufs=3))
 
-        w_planes = consts.tile([P, PASSES // PLANES_PER_TILE, FEATURES], U8, align_bytes=64)
-        nc.vector.memset(w_planes[:].bitcast(I32), 0)
+        w_planes = []
+        for half in range(2):
+            planes = consts.tile([P, PASSES // PLANES_PER_TILE, half_f], U8, name="w_planes_%d" % half, align_bytes=64)
+            nc.vector.memset(planes[:].bitcast(I32), 0)
+            w_planes.append(planes)
 
-        h_sb = consts.tile([P, K], BF16)
+        h_sb = []
         for pair in range(PASSES // 2):
-            cols = slice(2 * K_PASS * pair, 2 * K_PASS * (pair + 1))
-            nc.sync.dma_start(out=h_sb[:, cols], in_=h_rows[:, cols])
+            h_piece = consts.tile([P, 2 * K_PASS], BF16, name="h_sb_%d" % pair)
+            nc.sync.dma_start(out=h_piece[:], in_=h_rows[:, 2 * K_PASS * pair : 2 * K_PASS * (pair + 1)])
+            h_sb.append(h_piece)
 
-        for half in range(PASSES // PLANES_PER_TILE):
-            for quad in range(4):
+        banks = []
+        first = 0
+        for width in range_widths:
+            if first % half_f == 0:
+                for group in range(PASSES // PLANES_PER_TILE):
+                    for quad in range(4):
+                        nc.sync.dma_start(
+                            out=w_planes[first // half_f][32 * quad : 32 * quad + 16, group, :].bitcast(I32),
+                            in_=w_scale_rows[
+                                4 * group : 4 * group + 4, 4 * quad : 4 * quad + 4, first // 4 : (first + half_f) // 4
+                            ],
+                        )
+            passes_per_piece = PIECE_WORDS // width
+            pieces = []
+            for g in range(0, PASSES, passes_per_piece):
+                piece = weights.tile([P, passes_per_piece, width], U32, name="w_%d_%d" % (first, g), align_bytes=64)
                 nc.sync.dma_start(
-                    out=w_planes[32 * quad : 32 * quad + 16, half, :].bitcast(I32),
-                    in_=w_scale_rows[4 * half : 4 * half + 4, 4 * quad : 4 * quad + 4, :],
+                    out=piece[:].bitcast(I32), in_=w_words[:, g : g + passes_per_piece, first : first + width]
                 )
-
-        w_codes = []
-        for r in range(RANGES):
-            range_codes = weights.tile([P, PASSES, RANGE_F], U32, name="w_codes_%d" % r, align_bytes=64)
-            for g in range(PASSES):
-                nc.sync.dma_start(
-                    out=range_codes[:, g, :].bitcast(I32), in_=w_words[:, g, RANGE_F * r : RANGE_F * (r + 1)]
-                )
-            w_codes.append(range_codes)
+                pieces.append(piece)
+            bank_f = min(width, BANK_F)
+            for col in range(0, width, bank_f):
+                banks.append((pieces, col, first + col, bank_f))
+            first += width
+        n_banks = len(banks)
 
         gb_rows = consts.tile([P, P], BF16)
         nc.vector.memset(gb_rows[:], 0.0)
@@ -109,23 +138,13 @@ def tile_graphconvolutionbatch_w_kernel(tc, H, W_words, W_scales, gamma, beta, o
         gb = consts.tile([P, 2 * N_TILES], F32)
         aggregation = consts.tile([P, P], F32)
         with tc.psum_pool(name="head_psum", bufs=1) as head_psum:
-            h_pairs = h_sb[:].bitcast(F32)
+            scaled_flipped = head_psum.tile([P, P], F32)
+            nc.tensor.transpose(scaled_flipped[:], scaled_once[:], ident[:])
+            nc.vector.tensor_scalar_mul(out=aggregation[:], in0=scaled_flipped[:], scalar1=d[:, 0:1])
+
             grouped_pairs = grouped[:].bitcast(F32)
-            for pair in range(PASSES // 2):
-                flipped = head_psum.tile([P, 2, 2, P], F32, name="flipped_%d" % pair)
-                for gg in range(2):
-                    g = 2 * pair + gg
-                    for u in range(2):
-                        nc.tensor.transpose(
-                            flipped[:, gg, u, :], h_pairs[:, 256 * g + u : 256 * (g + 1) : 2], ident[:]
-                        )
-                dst = grouped_pairs[:, 2 * pair : 2 * pair + 2, :, :]
-                src = flipped[:].rearrange("p g u r -> p g r u")
-                if pair % 2 == 0:
-                    nc.vector.tensor_copy(out=dst, in_=src)
-                else:
-                    nc.scalar.copy(out=dst, in_=src)
-            for pair in range(PASSES // 2):
+
+            def quantise(pair):
                 gs = slice(2 * pair, 2 * pair + 2)
                 nc.vector.quantize_mx(
                     out=h_codes[:, gs, :].rearrange("p g r -> p (g r)").bitcast(FP8X4),
@@ -133,63 +152,86 @@ def tile_graphconvolutionbatch_w_kernel(tc, H, W_words, W_scales, gamma, beta, o
                     in_=grouped[:, gs, :, :].rearrange("p g r t -> p (g r t)"),
                 )
 
+            for pair in range(PASSES // 2):
+                flipped = head_psum.tile([P, 2, 2, P], F32, name="flipped_%d" % pair)
+                h_pairs = h_sb[pair][:].bitcast(F32)
+                for gg in range(2):
+                    for u in range(2):
+                        nc.tensor.transpose(
+                            flipped[:, gg, u, :], h_pairs[:, 256 * gg + u : 256 * (gg + 1) : 2], ident[:]
+                        )
+                dst = grouped_pairs[:, 2 * pair : 2 * pair + 2, :, :]
+                src = flipped[:].rearrange("p g u r -> p g r u")
+                if pair % 2 == 0:
+                    nc.vector.tensor_copy(out=dst, in_=src)
+                else:
+                    nc.scalar.copy(out=dst, in_=src)
+                if pair >= 1:
+                    quantise(pair - 1)
+            quantise(PASSES // 2 - 1)
+
             gb_rows_f32 = consts.tile([P, P], F32)
             nc.vector.tensor_copy(out=gb_rows_f32[:], in_=gb_rows[:])
             gb_flipped = head_psum.tile([P, P], F32)
             nc.tensor.transpose(gb_flipped[:], gb_rows_f32[:], ident[:])
             nc.vector.tensor_copy(out=gb[:], in_=gb_flipped[:, 0 : 2 * N_TILES])
 
-            scaled_flipped = head_psum.tile([P, P], F32)
-            nc.tensor.transpose(scaled_flipped[:], scaled_once[:], ident[:])
-            nc.vector.tensor_scalar_mul(out=aggregation[:], in0=scaled_flipped[:], scalar1=d[:, 0:1])
+        psum = ctx.enter_context(tc.psum_pool(name="psum", bufs=2))
+        acc = {}
+        y_rows = {}
+        normed = {}
+        z_rows = {}
 
-        acc_psum = ctx.enter_context(tc.psum_pool(name="acc_psum", bufs=2 * RANGE_BANKS))
-        flip_psum = ctx.enter_context(tc.psum_pool(name="flip_psum", bufs=1))
-        agg_psum = ctx.enter_context(tc.psum_pool(name="agg_psum", bufs=2))
-
-        def multiply(r):
-            sums = [acc_psum.tile([P, BANK_F], F32, name="acc") for b in range(RANGE_BANKS)]
-            for g in range(PASSES):
+        def multiply(n, passes):
+            pieces, col, first_f, bank_f = banks[n]
+            passes_per_piece = PASSES // len(pieces)
+            planes = w_planes[first_f // half_f]
+            plane_col = first_f % half_f
+            if n not in acc:
+                acc[n] = psum.tile([P, BANK_F], F32, name="acc")
+            for g in passes:
                 offset = 4 * (g % PLANES_PER_TILE)
-                for b in range(RANGE_BANKS):
-                    first = RANGE_F * r + BANK_F * b
-                    nc.tensor.matmul_mx(
-                        out=sums[b][:],
-                        lhsT=h_codes[:, g, :].bitcast(FP8X4),
-                        lhsT_scale=h_scales[:, g, :],
-                        rhs=w_codes[r][:, g, BANK_F * b : BANK_F * (b + 1)].bitcast(FP8X4),
-                        rhs_scale=w_planes[offset:P, g // PLANES_PER_TILE, first : first + BANK_F],
-                        start=(g == 0),
-                        stop=(g == PASSES - 1),
-                    )
-            return sums
+                nc.tensor.matmul_mx(
+                    out=acc[n][:, 0:bank_f],
+                    lhsT=h_codes[:, g, :].bitcast(FP8X4),
+                    lhsT_scale=h_scales[:, g, :],
+                    rhs=pieces[g // passes_per_piece][:, g % passes_per_piece, col : col + bank_f].bitcast(FP8X4),
+                    rhs_scale=planes[offset:P, g // PLANES_PER_TILE, plane_col : plane_col + bank_f],
+                    start=(g == 0),
+                    stop=(g == PASSES - 1),
+                )
 
-        def finish(bank, acc):
-            y_rows = work.tile([P, BANK_F], F32)
-            nc.scalar.copy(out=y_rows[:], in_=acc[:])
-            y_feat = flip_psum.tile([P, TILES_PER_BANK, P], F32)
-            for i in range(TILES_PER_BANK):
-                nc.tensor.transpose(y_feat[:, i, :], y_rows[:, P * i : P * (i + 1)], ident[:])
+        def copy_out(n):
+            bank_f = banks[n][3]
+            y_rows[n] = work.tile([P, BANK_F], F32, name="y_rows")
+            nc.scalar.copy(out=y_rows[n][:, 0:bank_f], in_=acc[n][:, 0:bank_f])
 
-            stats = small.tile([P, TILES_PER_BANK, 6], F32)
-            mean_var = small.tile([P, TILES_PER_BANK, 2], F32)
-            for i in range(TILES_PER_BANK):
+        def norm_by_feature(n):
+            first_f, bank_f = banks[n][2], banks[n][3]
+            tiles = bank_f // P
+            y_feat = psum.tile([P, BANK_F // P, P], F32)
+            for i in range(tiles):
+                nc.tensor.transpose(y_feat[:, i, :], y_rows[n][:, P * i : P * (i + 1)], ident[:])
+            stats = small.tile([P, BANK_F // P, 6], F32)
+            mean_var = small.tile([P, BANK_F // P, 2], F32)
+            for i in range(tiles):
                 nc.vector.bn_stats(out=stats[:, i, :], in_=y_feat[:, i, :])
                 nc.vector.bn_aggr(out=mean_var[:, i, :], in_=stats[:, i, :])
-            std = small.tile([P, TILES_PER_BANK], F32)
-            nc.scalar.activation(out=std[:], in_=mean_var[:, :, 1], func=ACT.Sqrt, bias=eps_bn[:, 0:1])
-            gain = small.tile([P, TILES_PER_BANK], F32)
-            nc.vector.reciprocal(out=gain[:], in_=std[:])
-            first_tile = TILES_PER_BANK * bank
-            nc.vector.tensor_mul(out=gain[:], in0=gain[:], in1=gb[:, first_tile : first_tile + TILES_PER_BANK])
-            shift = small.tile([P, TILES_PER_BANK], F32)
-            nc.vector.tensor_mul(out=shift[:], in0=mean_var[:, :, 0], in1=gain[:])
-            first_beta = N_TILES + first_tile
-            nc.vector.tensor_sub(out=shift[:], in0=gb[:, first_beta : first_beta + TILES_PER_BANK], in1=shift[:])
-            normed = work.tile([P, TILES_PER_BANK, P], F32)
-            for i in range(TILES_PER_BANK):
+            std = small.tile([P, BANK_F // P], F32)
+            nc.scalar.activation(out=std[:, 0:tiles], in_=mean_var[:, 0:tiles, 1], func=ACT.Sqrt, bias=eps_bn[:, 0:1])
+            gain = small.tile([P, BANK_F // P], F32)
+            nc.vector.reciprocal(out=gain[:, 0:tiles], in_=std[:, 0:tiles])
+            t0 = first_f // P
+            nc.vector.tensor_mul(out=gain[:, 0:tiles], in0=gain[:, 0:tiles], in1=gb[:, t0 : t0 + tiles])
+            shift = small.tile([P, BANK_F // P], F32)
+            nc.vector.tensor_mul(out=shift[:, 0:tiles], in0=mean_var[:, 0:tiles, 0], in1=gain[:, 0:tiles])
+            nc.vector.tensor_sub(
+                out=shift[:, 0:tiles], in0=gb[:, N_TILES + t0 : N_TILES + t0 + tiles], in1=shift[:, 0:tiles]
+            )
+            normed[n] = work.tile([P, BANK_F // P, P], F32, name="normed")
+            for i in range(tiles):
                 nc.vector.tensor_scalar(
-                    out=normed[:, i, :],
+                    out=normed[n][:, i, :],
                     in0=y_feat[:, i, :],
                     scalar1=gain[:, i : i + 1],
                     scalar2=shift[:, i : i + 1],
@@ -197,19 +239,33 @@ def tile_graphconvolutionbatch_w_kernel(tc, H, W_words, W_scales, gamma, beta, o
                     op1=ALU.add,
                 )
 
-            normed_rows = flip_psum.tile([P, BANK_F], F32)
-            for i in range(TILES_PER_BANK):
-                nc.tensor.transpose(normed_rows[:, P * i : P * (i + 1)], normed[:, i, :], ident[:])
-            z_rows = work.tile([P, BANK_F], F32)
-            nc.scalar.activation(out=z_rows[:], in_=normed_rows[:], func=ACT.Relu)
+        def relu_by_row(n):
+            bank_f = banks[n][3]
+            normed_rows = psum.tile([P, BANK_F], F32)
+            for i in range(bank_f // P):
+                nc.tensor.transpose(normed_rows[:, P * i : P * (i + 1)], normed[n][:, i, :], ident[:])
+            z_rows[n] = work.tile([P, BANK_F], F32, name="z_rows")
+            nc.scalar.activation(out=z_rows[n][:, 0:bank_f], in_=normed_rows[:, 0:bank_f], func=ACT.Relu)
 
-            summed = agg_psum.tile([P, BANK_F], F32)
-            nc.tensor.matmul(out=summed[:], lhsT=aggregation[:], rhs=z_rows[:], start=True, stop=True)
-            result = work.tile([P, BANK_F], F32)
-            nc.scalar.copy(out=result[:], in_=summed[:])
-            nc.scalar.dma_start(out=out_rows[:, BANK_F * bank : BANK_F * (bank + 1)], in_=result[:])
+        def aggregate_and_store(n):
+            first_f, bank_f = banks[n][2], banks[n][3]
+            summed = psum.tile([P, BANK_F], F32)
+            nc.tensor.matmul(
+                out=summed[:, 0:bank_f], lhsT=aggregation[:], rhs=z_rows[n][:, 0:bank_f], start=True, stop=True
+            )
+            result = results.tile([P, bank_f], F32, name="result_%d" % n)
+            nc.scalar.copy(out=result[:], in_=summed[:, 0:bank_f])
+            nc.sync.dma_start(out=out_rows[:, first_f : first_f + bank_f], in_=result[:])
 
-        for r in range(RANGES):
-            sums = multiply(r)
-            for b in range(RANGE_BANKS):
-                finish(RANGE_BANKS * r + b, sums[b])
+        for n in range(n_banks + 2):
+            if n >= 2:
+                relu_by_row(n - 2)
+            if 1 <= n <= n_banks:
+                norm_by_feature(n - 1)
+            if n < n_banks:
+                multiply(n, range(0, EARLY_PASSES))
+            if n >= 2:
+                aggregate_and_store(n - 2)
+            if n < n_banks:
+                multiply(n, range(EARLY_PASSES, PASSES))
+                copy_out(n)

@@ -24,7 +24,7 @@ BANK_F = 512
 FIRST_F = 512
 LAST_F = 256
 PIECE_WORDS = 1024
-EARLY_PASSES = 2
+EARLY_PASSES = PASSES // 2
 N_TILES = FEATURES // P
 EPS_BN = 1e-5
 EPS_DEG = 1e-5
@@ -125,12 +125,8 @@ def tile_graphconvolutionbatch_w_kernel(tc, H, W_words, W_scales, gamma, beta, o
 
         degree = consts.tile([P, 1], F32)
         nc.vector.reduce_sum(out=degree[:], in_=neighbours_2d, axis=mybir.AxisListType.X)
-        d_sqrt = consts.tile([P, 1], F32)
-        nc.scalar.activation(out=d_sqrt[:], in_=degree[:], func=ACT.Sqrt, bias=eps_deg[:, 0:1])
         d = consts.tile([P, 1], F32)
-        nc.vector.reciprocal(out=d[:], in_=d_sqrt[:])
-        scaled_once = consts.tile([P, P], F32)
-        nc.vector.tensor_scalar_mul(out=scaled_once[:], in0=neighbours_2d, scalar1=d[:, 0:1])
+        nc.scalar.activation(out=d[:], in_=degree[:], func=ACT.Abs_reciprocal_sqrt, bias=eps_deg[:, 0:1])
 
         grouped = consts.tile([P, PASSES, P, PACK], BF16, align_bytes=64)
         h_codes = consts.tile([P, PASSES, P], U32, align_bytes=64)
@@ -138,10 +134,6 @@ def tile_graphconvolutionbatch_w_kernel(tc, H, W_words, W_scales, gamma, beta, o
         gb = consts.tile([P, 2 * N_TILES], F32)
         aggregation = consts.tile([P, P], F32)
         with tc.psum_pool(name="head_psum", bufs=1) as head_psum:
-            scaled_flipped = head_psum.tile([P, P], F32)
-            nc.tensor.transpose(scaled_flipped[:], scaled_once[:], ident[:])
-            nc.vector.tensor_scalar_mul(out=aggregation[:], in0=scaled_flipped[:], scalar1=d[:, 0:1])
-
             grouped_pairs = grouped[:].bitcast(F32)
 
             def quantise(pair):
@@ -176,9 +168,16 @@ def tile_graphconvolutionbatch_w_kernel(tc, H, W_words, W_scales, gamma, beta, o
             nc.tensor.transpose(gb_flipped[:], gb_rows_f32[:], ident[:])
             nc.vector.tensor_copy(out=gb[:], in_=gb_flipped[:, 0 : 2 * N_TILES])
 
+            scaled_once = consts.tile([P, P], F32)
+            nc.vector.tensor_scalar_mul(out=scaled_once[:], in0=neighbours_2d, scalar1=d[:, 0:1])
+            scaled_flipped = head_psum.tile([P, P], F32)
+            nc.tensor.transpose(scaled_flipped[:], scaled_once[:], ident[:])
+            nc.vector.tensor_scalar_mul(out=aggregation[:], in0=scaled_flipped[:], scalar1=d[:, 0:1])
+
         psum = ctx.enter_context(tc.psum_pool(name="psum", bufs=2))
         acc = {}
         y_rows = {}
+        y_feat = {}
         normed = {}
         z_rows = {}
 
@@ -206,25 +205,31 @@ def tile_graphconvolutionbatch_w_kernel(tc, H, W_words, W_scales, gamma, beta, o
             y_rows[n] = work.tile([P, BANK_F], F32, name="y_rows")
             nc.scalar.copy(out=y_rows[n][:, 0:bank_f], in_=acc[n][:, 0:bank_f])
 
-        def norm_by_feature(n):
+        def features_to_partitions(n):
+            y_feat[n] = psum.tile([P, BANK_F // P, P], F32, name="y_feat")
+            for i in range(banks[n][3] // P):
+                nc.tensor.transpose(y_feat[n][:, i, :], y_rows[n][:, P * i : P * (i + 1)], ident[:])
+
+        def batch_norm(n):
             first_f, bank_f = banks[n][2], banks[n][3]
             tiles = bank_f // P
-            y_feat = psum.tile([P, BANK_F // P, P], F32)
-            for i in range(tiles):
-                nc.tensor.transpose(y_feat[:, i, :], y_rows[n][:, P * i : P * (i + 1)], ident[:])
             stats = small.tile([P, BANK_F // P, 6], F32)
             mean_var = small.tile([P, BANK_F // P, 2], F32)
             for i in range(tiles):
-                nc.vector.bn_stats(out=stats[:, i, :], in_=y_feat[:, i, :])
+                nc.vector.bn_stats(out=stats[:, i, :], in_=y_feat[n][:, i, :])
+            for i in range(tiles):
                 nc.vector.bn_aggr(out=mean_var[:, i, :], in_=stats[:, i, :])
-            std = small.tile([P, BANK_F // P], F32)
-            nc.scalar.activation(out=std[:, 0:tiles], in_=mean_var[:, 0:tiles, 1], func=ACT.Sqrt, bias=eps_bn[:, 0:1])
-            gain = small.tile([P, BANK_F // P], F32)
-            nc.vector.reciprocal(out=gain[:, 0:tiles], in_=std[:, 0:tiles])
+            inv_std = small.tile([P, BANK_F // P], F32)
+            nc.scalar.activation(
+                out=inv_std[:, 0:tiles], in_=mean_var[:, 0:tiles, 1], func=ACT.Abs_reciprocal_sqrt, bias=eps_bn[:, 0:1]
+            )
             t0 = first_f // P
-            nc.vector.tensor_mul(out=gain[:, 0:tiles], in0=gain[:, 0:tiles], in1=gb[:, t0 : t0 + tiles])
+            mean_gamma = small.tile([P, BANK_F // P], F32)
+            nc.vector.tensor_mul(out=mean_gamma[:, 0:tiles], in0=mean_var[:, 0:tiles, 0], in1=gb[:, t0 : t0 + tiles])
             shift = small.tile([P, BANK_F // P], F32)
-            nc.vector.tensor_mul(out=shift[:, 0:tiles], in0=mean_var[:, 0:tiles, 0], in1=gain[:, 0:tiles])
+            nc.vector.tensor_mul(out=shift[:, 0:tiles], in0=mean_gamma[:, 0:tiles], in1=inv_std[:, 0:tiles])
+            gain = small.tile([P, BANK_F // P], F32)
+            nc.vector.tensor_mul(out=gain[:, 0:tiles], in0=inv_std[:, 0:tiles], in1=gb[:, t0 : t0 + tiles])
             nc.vector.tensor_sub(
                 out=shift[:, 0:tiles], in0=gb[:, N_TILES + t0 : N_TILES + t0 + tiles], in1=shift[:, 0:tiles]
             )
@@ -232,7 +237,7 @@ def tile_graphconvolutionbatch_w_kernel(tc, H, W_words, W_scales, gamma, beta, o
             for i in range(tiles):
                 nc.vector.tensor_scalar(
                     out=normed[n][:, i, :],
-                    in0=y_feat[:, i, :],
+                    in0=y_feat[n][:, i, :],
                     scalar1=gain[:, i : i + 1],
                     scalar2=shift[:, i : i + 1],
                     op0=ALU.mult,
@@ -258,14 +263,16 @@ def tile_graphconvolutionbatch_w_kernel(tc, H, W_words, W_scales, gamma, beta, o
             nc.sync.dma_start(out=out_rows[:, first_f : first_f + bank_f], in_=result[:])
 
         for n in range(n_banks + 2):
+            if n < n_banks:
+                multiply(n, range(0, EARLY_PASSES))
+            if 1 <= n <= n_banks:
+                features_to_partitions(n - 1)
             if n >= 2:
                 relu_by_row(n - 2)
             if 1 <= n <= n_banks:
-                norm_by_feature(n - 1)
-            if n < n_banks:
-                multiply(n, range(0, EARLY_PASSES))
-            if n >= 2:
-                aggregate_and_store(n - 2)
+                batch_norm(n - 1)
             if n < n_banks:
                 multiply(n, range(EARLY_PASSES, PASSES))
                 copy_out(n)
+            if n >= 2:
+                aggregate_and_store(n - 2)

@@ -21,25 +21,13 @@ K_PASS = P * PACK
 PASSES = K // K_PASS
 PLANES_PER_TILE = 4
 BANK_F = 512
-FIRST_F = 512
 LAST_F = 256
 PIECE_WORDS = 1024
-EARLY_PASSES = PASSES // 2
 N_TILES = FEATURES // P
 EPS_BN = 1e-5
 EPS_DEG = 1e-5
 
 FLOPS = 2 * P * K * FEATURES
-
-
-def halvings(total, smallest):
-    widths = []
-    left = total
-    while left > smallest:
-        left //= 2
-        widths.append(left)
-    widths.append(left)
-    return widths
 
 
 def tile_graphconvolutionbatch_w_kernel(tc, H, W_words, W_scales, gamma, beta, out):
@@ -50,7 +38,7 @@ def tile_graphconvolutionbatch_w_kernel(tc, H, W_words, W_scales, gamma, beta, o
     w_scale_rows = W_scales.bitcast(I32)
 
     half_f = FEATURES // 2
-    range_widths = list(reversed(halvings(half_f, FIRST_F))) + halvings(half_f, LAST_F)
+    range_widths = [BANK_F] * (FEATURES // BANK_F - 1) + [LAST_F] * (BANK_F // LAST_F)
 
     with ExitStack() as ctx:
         ctx.enter_context(tc.manual_schedule())
@@ -176,39 +164,30 @@ def tile_graphconvolutionbatch_w_kernel(tc, H, W_words, W_scales, gamma, beta, o
 
         psum = ctx.enter_context(tc.psum_pool(name="psum", bufs=2))
         acc = {}
-        y_rows = {}
-        y_feat = {}
         normed = {}
         z_rows = {}
 
-        def multiply(n, passes):
+        def multiply(n, tiles):
             pieces, col, first_f, bank_f = banks[n]
             passes_per_piece = PASSES // len(pieces)
             planes = w_planes[first_f // half_f]
             plane_col = first_f % half_f
             if n not in acc:
-                acc[n] = psum.tile([P, BANK_F], F32, name="acc")
-            for g in passes:
-                offset = 4 * (g % PLANES_PER_TILE)
-                nc.tensor.matmul_mx(
-                    out=acc[n][:, 0:bank_f],
-                    lhsT=h_codes[:, g, :].bitcast(FP8X4),
-                    lhsT_scale=h_scales[:, g, :],
-                    rhs=pieces[g // passes_per_piece][:, g % passes_per_piece, col : col + bank_f].bitcast(FP8X4),
-                    rhs_scale=planes[offset:P, g // PLANES_PER_TILE, plane_col : plane_col + bank_f],
-                    start=(g == 0),
-                    stop=(g == PASSES - 1),
-                )
-
-        def copy_out(n):
-            bank_f = banks[n][3]
-            y_rows[n] = work.tile([P, BANK_F], F32, name="y_rows")
-            nc.scalar.copy(out=y_rows[n][:, 0:bank_f], in_=acc[n][:, 0:bank_f])
-
-        def features_to_partitions(n):
-            y_feat[n] = psum.tile([P, BANK_F // P, P], F32, name="y_feat")
-            for i in range(banks[n][3] // P):
-                nc.tensor.transpose(y_feat[n][:, i, :], y_rows[n][:, P * i : P * (i + 1)], ident[:])
+                acc[n] = psum.tile([P, BANK_F // P, P], F32, name="acc")
+            for i in tiles:
+                for g in range(PASSES):
+                    offset = 4 * (g % PLANES_PER_TILE)
+                    nc.tensor.matmul_mx(
+                        out=acc[n][:, i, :],
+                        lhsT=pieces[g // passes_per_piece][
+                            :, g % passes_per_piece, col + P * i : col + P * (i + 1)
+                        ].bitcast(FP8X4),
+                        lhsT_scale=planes[offset:P, g // PLANES_PER_TILE, plane_col + P * i : plane_col + P * (i + 1)],
+                        rhs=h_codes[:, g, :].bitcast(FP8X4),
+                        rhs_scale=h_scales[:, g, :],
+                        start=(g == 0),
+                        stop=(g == PASSES - 1),
+                    )
 
         def batch_norm(n):
             first_f, bank_f = banks[n][2], banks[n][3]
@@ -216,7 +195,7 @@ def tile_graphconvolutionbatch_w_kernel(tc, H, W_words, W_scales, gamma, beta, o
             stats = small.tile([P, BANK_F // P, 6], F32)
             mean_var = small.tile([P, BANK_F // P, 2], F32)
             for i in range(tiles):
-                nc.vector.bn_stats(out=stats[:, i, :], in_=y_feat[n][:, i, :])
+                nc.vector.bn_stats(out=stats[:, i, :], in_=acc[n][:, i, :])
             for i in range(tiles):
                 nc.vector.bn_aggr(out=mean_var[:, i, :], in_=stats[:, i, :])
             inv_std = small.tile([P, BANK_F // P], F32)
@@ -237,7 +216,7 @@ def tile_graphconvolutionbatch_w_kernel(tc, H, W_words, W_scales, gamma, beta, o
             for i in range(tiles):
                 nc.vector.tensor_scalar(
                     out=normed[n][:, i, :],
-                    in0=y_feat[n][:, i, :],
+                    in0=acc[n][:, i, :],
                     scalar1=gain[:, i : i + 1],
                     scalar2=shift[:, i : i + 1],
                     op0=ALU.mult,
@@ -264,15 +243,12 @@ def tile_graphconvolutionbatch_w_kernel(tc, H, W_words, W_scales, gamma, beta, o
 
         for n in range(n_banks + 2):
             if n < n_banks:
-                multiply(n, range(0, EARLY_PASSES))
-            if 1 <= n <= n_banks:
-                features_to_partitions(n - 1)
+                tiles = banks[n][3] // P
+                multiply(n, range(0, tiles // 2))
             if n >= 2:
                 relu_by_row(n - 2)
-            if 1 <= n <= n_banks:
-                batch_norm(n - 1)
             if n < n_banks:
-                multiply(n, range(EARLY_PASSES, PASSES))
-                copy_out(n)
+                multiply(n, range(tiles // 2, tiles))
+                batch_norm(n)
             if n >= 2:
                 aggregate_and_store(n - 2)

@@ -35,9 +35,8 @@ def tile_graphconvolutionbatch_w_kernel(tc, H, W_words, W_scales, gamma, beta, o
     h_rows = H.rearrange("b n k -> (b n) k")
     out_rows = out.rearrange("b n f -> (b n) f")
     w_words = W_words.rearrange("g p n t -> g p (n t)").bitcast(I32).rearrange("g p n -> p g n")
-    w_scale_rows = W_scales.bitcast(I32)
+    w_scale_rows = W_scales.bitcast(F32)
 
-    half_f = FEATURES // 2
     range_widths = [BANK_F] * (FEATURES // BANK_F - 1) + [LAST_F] * (BANK_F // LAST_F)
 
     with ExitStack() as ctx:
@@ -48,11 +47,8 @@ def tile_graphconvolutionbatch_w_kernel(tc, H, W_words, W_scales, gamma, beta, o
         small = ctx.enter_context(tc.tile_pool(name="small", bufs=4))
         work = ctx.enter_context(tc.tile_pool(name="work", bufs=3))
 
-        w_planes = []
-        for half in range(2):
-            planes = consts.tile([P, PASSES // PLANES_PER_TILE, half_f], U8, name="w_planes_%d" % half, align_bytes=64)
-            nc.vector.memset(planes[:].bitcast(I32), 0)
-            w_planes.append(planes)
+        w_planes = consts.tile([P, PASSES // PLANES_PER_TILE, FEATURES], U8, align_bytes=64)
+        nc.vector.memset(w_planes[:].bitcast(I32), 0)
 
         h_sb = []
         for pair in range(PASSES // 2):
@@ -63,15 +59,6 @@ def tile_graphconvolutionbatch_w_kernel(tc, H, W_words, W_scales, gamma, beta, o
         banks = []
         first = 0
         for width in range_widths:
-            if first % half_f == 0:
-                for group in range(PASSES // PLANES_PER_TILE):
-                    for quad in range(4):
-                        nc.sync.dma_start(
-                            out=w_planes[first // half_f][32 * quad : 32 * quad + 16, group, :].bitcast(I32),
-                            in_=w_scale_rows[
-                                4 * group : 4 * group + 4, 4 * quad : 4 * quad + 4, first // 4 : (first + half_f) // 4
-                            ],
-                        )
             passes_per_piece = PIECE_WORDS // width
             pieces = []
             for g in range(0, PASSES, passes_per_piece):
@@ -93,6 +80,13 @@ def tile_graphconvolutionbatch_w_kernel(tc, H, W_words, W_scales, gamma, beta, o
 
         ident = consts.tile([P, P], F32)
         make_identity(nc, ident[:])
+
+        for group in range(PASSES // PLANES_PER_TILE):
+            for quad in (0, 2, 1, 3):
+                nc.gpsimd.dma_start(
+                    out=w_planes[32 * quad : 32 * quad + 16, group, :].bitcast(F32),
+                    in_=w_scale_rows[4 * group : 4 * group + 4, 4 * quad : 4 * quad + 4, :],
+                )
         eps_bn = consts.tile([P, 1], F32)
         nc.vector.memset(eps_bn[:], EPS_BN)
         eps_deg = consts.tile([P, 1], F32)
@@ -170,8 +164,6 @@ def tile_graphconvolutionbatch_w_kernel(tc, H, W_words, W_scales, gamma, beta, o
         def multiply(n, tiles):
             pieces, col, first_f, bank_f = banks[n]
             passes_per_piece = PASSES // len(pieces)
-            planes = w_planes[first_f // half_f]
-            plane_col = first_f % half_f
             if n not in acc:
                 acc[n] = psum.tile([P, BANK_F // P, P], F32, name="acc")
             for i in tiles:
@@ -182,7 +174,7 @@ def tile_graphconvolutionbatch_w_kernel(tc, H, W_words, W_scales, gamma, beta, o
                         lhsT=pieces[g // passes_per_piece][
                             :, g % passes_per_piece, col + P * i : col + P * (i + 1)
                         ].bitcast(FP8X4),
-                        lhsT_scale=planes[offset:P, g // PLANES_PER_TILE, plane_col + P * i : plane_col + P * (i + 1)],
+                        lhsT_scale=w_planes[offset:P, g // PLANES_PER_TILE, first_f + P * i : first_f + P * (i + 1)],
                         rhs=h_codes[:, g, :].bitcast(FP8X4),
                         rhs_scale=h_scales[:, g, :],
                         start=(g == 0),

@@ -114,7 +114,8 @@ def tile_graphconvolutionbatch_w_kernel(tc, H, W_words, W_scales, gamma, beta, o
         h_codes = consts.tile([P, PASSES, P], U32, align_bytes=64)
         h_scales = consts.tile([P, PASSES, P], U8, align_bytes=64)
         gb = consts.tile([P, 2 * N_TILES], F32)
-        aggregation = consts.tile([P, P], F32)
+        neighbours_bf = consts.tile([P, P], BF16)
+        nc.vector.tensor_copy(out=neighbours_bf[:], in_=neighbours_2d)
         with tc.psum_pool(name="head_psum", bufs=1) as head_psum:
             grouped_pairs = grouped[:].bitcast(F32)
 
@@ -150,16 +151,19 @@ def tile_graphconvolutionbatch_w_kernel(tc, H, W_words, W_scales, gamma, beta, o
             nc.tensor.transpose(gb_flipped[:], gb_rows_f32[:], ident[:])
             nc.vector.tensor_copy(out=gb[:], in_=gb_flipped[:, 0 : 2 * N_TILES])
 
-            scaled_once = consts.tile([P, P], F32)
-            nc.vector.tensor_scalar_mul(out=scaled_once[:], in0=neighbours_2d, scalar1=d[:, 0:1])
-            scaled_flipped = head_psum.tile([P, P], F32)
-            nc.tensor.transpose(scaled_flipped[:], scaled_once[:], ident[:])
-            nc.vector.tensor_scalar_mul(out=aggregation[:], in0=scaled_flipped[:], scalar1=d[:, 0:1])
 
         psum = ctx.enter_context(tc.psum_pool(name="psum", bufs=2))
         acc = {}
-        normed = {}
-        z_rows = {}
+        mean_var = {}
+        mean_gamma = {}
+        inv_std = {}
+        gain = {}
+        shift = {}
+        z_feat = {}
+        z_psum = {}
+        z_high = {}
+        z_low = {}
+        summed = {}
 
         def multiply(n, tiles):
             pieces, col, first_f, bank_f = banks[n]
@@ -181,66 +185,111 @@ def tile_graphconvolutionbatch_w_kernel(tc, H, W_words, W_scales, gamma, beta, o
                         stop=(g == PASSES - 1),
                     )
 
-        def batch_norm(n):
+        def statistics(n):
             first_f, bank_f = banks[n][2], banks[n][3]
             tiles = bank_f // P
+            t0 = first_f // P
             stats = small.tile([P, BANK_F // P, 6], F32)
-            mean_var = small.tile([P, BANK_F // P, 2], F32)
+            mean_var[n] = small.tile([P, BANK_F // P, 2], F32, name="mean_var")
             for i in range(tiles):
                 nc.vector.bn_stats(out=stats[:, i, :], in_=acc[n][:, i, :])
             for i in range(tiles):
-                nc.vector.bn_aggr(out=mean_var[:, i, :], in_=stats[:, i, :])
-            inv_std = small.tile([P, BANK_F // P], F32)
+                nc.vector.bn_aggr(out=mean_var[n][:, i, :], in_=stats[:, i, :])
+            mean_gamma[n] = small.tile([P, BANK_F // P], F32, name="mean_gamma")
+            nc.vector.tensor_mul(
+                out=mean_gamma[n][:, 0:tiles], in0=mean_var[n][:, 0:tiles, 0], in1=gb[:, t0 : t0 + tiles]
+            )
+
+        def inverse_deviation(n):
+            tiles = banks[n][3] // P
+            inv_std[n] = small.tile([P, BANK_F // P], F32, name="inv_std")
             nc.scalar.activation(
-                out=inv_std[:, 0:tiles], in_=mean_var[:, 0:tiles, 1], func=ACT.Abs_reciprocal_sqrt, bias=eps_bn[:, 0:1]
+                out=inv_std[n][:, 0:tiles],
+                in_=mean_var[n][:, 0:tiles, 1],
+                func=ACT.Abs_reciprocal_sqrt,
+                bias=eps_bn[:, 0:1],
             )
+
+        def gain_and_shift(n):
+            first_f, bank_f = banks[n][2], banks[n][3]
+            tiles = bank_f // P
             t0 = first_f // P
-            mean_gamma = small.tile([P, BANK_F // P], F32)
-            nc.vector.tensor_mul(out=mean_gamma[:, 0:tiles], in0=mean_var[:, 0:tiles, 0], in1=gb[:, t0 : t0 + tiles])
-            shift = small.tile([P, BANK_F // P], F32)
-            nc.vector.tensor_mul(out=shift[:, 0:tiles], in0=mean_gamma[:, 0:tiles], in1=inv_std[:, 0:tiles])
-            gain = small.tile([P, BANK_F // P], F32)
-            nc.vector.tensor_mul(out=gain[:, 0:tiles], in0=inv_std[:, 0:tiles], in1=gb[:, t0 : t0 + tiles])
+            shift[n] = small.tile([P, BANK_F // P], F32, name="shift")
+            nc.vector.tensor_mul(out=shift[n][:, 0:tiles], in0=mean_gamma[n][:, 0:tiles], in1=inv_std[n][:, 0:tiles])
+            gain[n] = small.tile([P, BANK_F // P], F32, name="gain")
+            nc.vector.tensor_mul(out=gain[n][:, 0:tiles], in0=inv_std[n][:, 0:tiles], in1=gb[:, t0 : t0 + tiles])
             nc.vector.tensor_sub(
-                out=shift[:, 0:tiles], in0=gb[:, N_TILES + t0 : N_TILES + t0 + tiles], in1=shift[:, 0:tiles]
+                out=shift[n][:, 0:tiles], in0=gb[:, N_TILES + t0 : N_TILES + t0 + tiles], in1=shift[n][:, 0:tiles]
             )
-            normed[n] = work.tile([P, BANK_F // P, P], F32, name="normed")
-            for i in range(tiles):
-                nc.vector.tensor_scalar(
-                    out=normed[n][:, i, :],
-                    in0=acc[n][:, i, :],
-                    scalar1=gain[:, i : i + 1],
-                    scalar2=shift[:, i : i + 1],
-                    op0=ALU.mult,
-                    op1=ALU.add,
+
+        def norm_and_relu(n):
+            z_feat[n] = work.tile([P, BANK_F // P, P], F32, name="z_feat")
+            for i in range(banks[n][3] // P):
+                nc.scalar.activation(
+                    out=z_feat[n][:, i, :],
+                    in_=acc[n][:, i, :],
+                    func=ACT.Relu,
+                    scale=gain[n][:, i : i + 1],
+                    bias=shift[n][:, i : i + 1],
                 )
 
-        def relu_by_row(n):
-            bank_f = banks[n][3]
-            normed_rows = psum.tile([P, BANK_F], F32)
-            for i in range(bank_f // P):
-                nc.tensor.transpose(normed_rows[:, P * i : P * (i + 1)], normed[n][:, i, :], ident[:])
-            z_rows[n] = work.tile([P, BANK_F], F32, name="z_rows")
-            nc.scalar.activation(out=z_rows[n][:, 0:bank_f], in_=normed_rows[:, 0:bank_f], func=ACT.Relu)
+        def to_rows(n):
+            z_psum[n] = psum.tile([P, BANK_F], F32, name="z_psum")
+            for i in range(banks[n][3] // P):
+                nc.tensor.transpose(z_psum[n][:, P * i : P * (i + 1)], z_feat[n][:, i, :], ident[:])
 
-        def aggregate_and_store(n):
-            first_f, bank_f = banks[n][2], banks[n][3]
-            summed = psum.tile([P, BANK_F], F32)
-            nc.tensor.matmul(
-                out=summed[:, 0:bank_f], lhsT=aggregation[:], rhs=z_rows[n][:, 0:bank_f], start=True, stop=True
+        def split_high(n):
+            bank_f = banks[n][3]
+            z_high[n] = work.tile([P, BANK_F], BF16, name="z_high")
+            nc.scalar.activation(
+                out=z_high[n][:, 0:bank_f], in_=z_psum[n][:, 0:bank_f], func=ACT.Copy, scale=d[:, 0:1]
             )
+
+        def split_low(n):
+            bank_f = banks[n][3]
+            z_low[n] = work.tile([P, BANK_F], BF16, name="z_low")
+            nc.vector.scalar_tensor_tensor(
+                out=z_low[n][:, 0:bank_f],
+                in0=z_psum[n][:, 0:bank_f],
+                scalar=d[:, 0:1],
+                in1=z_high[n][:, 0:bank_f],
+                op0=ALU.mult,
+                op1=ALU.subtract,
+            )
+
+        def aggregate(n):
+            bank_f = banks[n][3]
+            summed[n] = psum.tile([P, BANK_F], F32, name="summed")
+            nc.tensor.matmul(
+                out=summed[n][:, 0:bank_f], lhsT=neighbours_bf[:], rhs=z_high[n][:, 0:bank_f], start=True, stop=False
+            )
+            nc.tensor.matmul(
+                out=summed[n][:, 0:bank_f], lhsT=neighbours_bf[:], rhs=z_low[n][:, 0:bank_f], start=False, stop=True
+            )
+
+        def store(n):
+            first_f, bank_f = banks[n][2], banks[n][3]
             result = results.tile([P, bank_f], F32, name="result_%d" % n)
-            nc.scalar.copy(out=result[:], in_=summed[:, 0:bank_f])
+            nc.vector.tensor_scalar_mul(out=result[:], in0=summed[n][:, 0:bank_f], scalar1=d[:, 0:1])
             nc.sync.dma_start(out=out_rows[:, first_f : first_f + bank_f], in_=result[:])
 
         for n in range(n_banks + 2):
             if n < n_banks:
                 tiles = banks[n][3] // P
-                multiply(n, range(0, tiles // 2))
+                multiply(n, range(0, 1))
             if n >= 2:
-                relu_by_row(n - 2)
+                to_rows(n - 2)
+                split_high(n - 2)
+            if 1 <= n <= n_banks:
+                norm_and_relu(n - 1)
+            if n >= 2:
+                split_low(n - 2)
             if n < n_banks:
-                multiply(n, range(tiles // 2, tiles))
-                batch_norm(n)
+                multiply(n, range(1, tiles))
+                statistics(n)
+                inverse_deviation(n)
             if n >= 2:
-                aggregate_and_store(n - 2)
+                aggregate(n - 2)
+                store(n - 2)
+            if n < n_banks:
+                gain_and_shift(n)

@@ -22,7 +22,6 @@ PASSES = K // K_PASS
 PLANES_PER_TILE = 4
 BANK_F = 512
 LAST_F = 256
-PIECE_WORDS = 1024
 N_TILES = FEATURES // P
 EPS_BN = 1e-5
 EPS_DEG = 1e-5
@@ -38,6 +37,7 @@ def tile_graphconvolutionbatch_w_kernel(tc, H, W_words, W_scales, gamma, beta, o
     w_scale_rows = W_scales.bitcast(F32)
 
     range_widths = [BANK_F] * (FEATURES // BANK_F - 1) + [LAST_F] * (BANK_F // LAST_F)
+    range_pieces = [[2, 2, 2, 2]] * (FEATURES // BANK_F - 1) + [[4, 4], [4, 3, 1]]
 
     with ExitStack() as ctx:
         ctx.enter_context(tc.manual_schedule())
@@ -58,18 +58,14 @@ def tile_graphconvolutionbatch_w_kernel(tc, H, W_words, W_scales, gamma, beta, o
 
         banks = []
         first = 0
-        for width in range_widths:
-            passes_per_piece = PIECE_WORDS // width
-            pieces = []
-            for g in range(0, PASSES, passes_per_piece):
-                piece = weights.tile([P, passes_per_piece, width], U32, name="w_%d_%d" % (first, g), align_bytes=64)
-                nc.sync.dma_start(
-                    out=piece[:].bitcast(I32), in_=w_words[:, g : g + passes_per_piece, first : first + width]
-                )
-                pieces.append(piece)
-            bank_f = min(width, BANK_F)
-            for col in range(0, width, bank_f):
-                banks.append((pieces, col, first + col, bank_f))
+        for width, pieces in zip(range_widths, range_pieces):
+            words = []
+            for passes in pieces:
+                g = len(words)
+                piece = weights.tile([P, passes, width], U32, name="w_%d_%d" % (first, g), align_bytes=64)
+                nc.sync.dma_start(out=piece[:].bitcast(I32), in_=w_words[:, g : g + passes, first : first + width])
+                words.extend([piece[:, j, :] for j in range(passes)])
+            banks.append((words, pieces[0], first, width))
             first += width
         n_banks = len(banks)
 
@@ -165,25 +161,36 @@ def tile_graphconvolutionbatch_w_kernel(tc, H, W_words, W_scales, gamma, beta, o
         z_low = {}
         summed = {}
 
-        def multiply(n, tiles):
-            pieces, col, first_f, bank_f = banks[n]
-            passes_per_piece = PASSES // len(pieces)
+        def one_pass(n, i, g):
+            words, first_f = banks[n][0], banks[n][2]
+            offset = 4 * (g % PLANES_PER_TILE)
+            nc.tensor.matmul_mx(
+                out=acc[n][i],
+                lhsT=words[g][:, P * i : P * (i + 1)].bitcast(FP8X4),
+                lhsT_scale=w_planes[offset:P, g // PLANES_PER_TILE, first_f + P * i : first_f + P * (i + 1)],
+                rhs=h_codes[:, g, :].bitcast(FP8X4),
+                rhs_scale=h_scales[:, g, :],
+                start=(g == 0),
+                stop=(g == PASSES - 1),
+            )
+
+        def multiply_by_tile(n, tiles):
             if n not in acc:
-                acc[n] = psum.tile([P, BANK_F // P, P], F32, name="acc")
+                bank = psum.tile([P, BANK_F // P, P], F32, name="acc", bufs=4)
+                acc[n] = [bank[:, i, :] for i in range(BANK_F // P)]
             for i in tiles:
                 for g in range(PASSES):
-                    offset = 4 * (g % PLANES_PER_TILE)
-                    nc.tensor.matmul_mx(
-                        out=acc[n][:, i, :],
-                        lhsT=pieces[g // passes_per_piece][
-                            :, g % passes_per_piece, col + P * i : col + P * (i + 1)
-                        ].bitcast(FP8X4),
-                        lhsT_scale=w_planes[offset:P, g // PLANES_PER_TILE, first_f + P * i : first_f + P * (i + 1)],
-                        rhs=h_codes[:, g, :].bitcast(FP8X4),
-                        rhs_scale=h_scales[:, g, :],
-                        start=(g == 0),
-                        stop=(g == PASSES - 1),
-                    )
+                    one_pass(n, i, g)
+
+        def multiply_by_pass(n, passes):
+            if n not in acc:
+                acc[n] = []
+                for i in range(banks[n][3] // P):
+                    bank = psum.tile([P, BANK_F // P, P], F32, name="acc", bufs=4)
+                    acc[n].append(bank[:, 0, :])
+            for g in passes:
+                for i in range(banks[n][3] // P):
+                    one_pass(n, i, g)
 
         def statistics(n):
             first_f, bank_f = banks[n][2], banks[n][3]
@@ -192,7 +199,7 @@ def tile_graphconvolutionbatch_w_kernel(tc, H, W_words, W_scales, gamma, beta, o
             stats = small.tile([P, BANK_F // P, 6], F32)
             mean_var[n] = small.tile([P, BANK_F // P, 2], F32, name="mean_var")
             for i in range(tiles):
-                nc.vector.bn_stats(out=stats[:, i, :], in_=acc[n][:, i, :])
+                nc.vector.bn_stats(out=stats[:, i, :], in_=acc[n][i])
             for i in range(tiles):
                 nc.vector.bn_aggr(out=mean_var[n][:, i, :], in_=stats[:, i, :])
             mean_gamma[n] = small.tile([P, BANK_F // P], F32, name="mean_gamma")
@@ -227,7 +234,7 @@ def tile_graphconvolutionbatch_w_kernel(tc, H, W_words, W_scales, gamma, beta, o
             for i in range(banks[n][3] // P):
                 nc.scalar.activation(
                     out=z_feat[n][:, i, :],
-                    in_=acc[n][:, i, :],
+                    in_=acc[n][i],
                     func=ACT.Relu,
                     scale=gain[n][:, i : i + 1],
                     bias=shift[n][:, i : i + 1],
@@ -275,8 +282,11 @@ def tile_graphconvolutionbatch_w_kernel(tc, H, W_words, W_scales, gamma, beta, o
 
         for n in range(n_banks + 2):
             if n < n_banks:
-                tiles = banks[n][3] // P
-                multiply(n, range(0, 1))
+                by_pass = banks[n][3] < BANK_F
+                if by_pass:
+                    multiply_by_pass(n, range(0, banks[n][1]))
+                else:
+                    multiply_by_tile(n, range(0, 1))
             if n >= 2:
                 to_rows(n - 2)
                 split_high(n - 2)
@@ -285,7 +295,10 @@ def tile_graphconvolutionbatch_w_kernel(tc, H, W_words, W_scales, gamma, beta, o
             if n >= 2:
                 split_low(n - 2)
             if n < n_banks:
-                multiply(n, range(1, tiles))
+                if by_pass:
+                    multiply_by_pass(n, range(banks[n][1], PASSES))
+                else:
+                    multiply_by_tile(n, range(1, BANK_F // P))
                 statistics(n)
                 inverse_deviation(n)
             if n >= 2:

@@ -281,24 +281,13 @@ def tile_graphconvolutionbatch_w_kernel(tc, H, W_words, W_scales, gamma, beta, o
             nc.sync.dma_start(out=out_rows[:, first_f : first_f + bank_f], in_=result[:])
 
         for n in range(n_banks + 2):
-            if n < n_banks:
-                by_pass = banks[n][3] < BANK_F
-                if by_pass:
-                    multiply_by_pass(n, range(0, banks[n][1]))
-                else:
-                    multiply_by_tile(n, range(0, 1))
-            if n >= 2:
-                to_rows(n - 2)
-                split_high(n - 2)
             if 1 <= n <= n_banks:
                 norm_and_relu(n - 1)
-            if n >= 2:
-                split_low(n - 2)
             if n < n_banks:
-                if by_pass:
-                    multiply_by_pass(n, range(banks[n][1], PASSES))
+                if banks[n][3] < BANK_F:
+                    multiply_by_pass(n, range(PASSES))
                 else:
-                    multiply_by_tile(n, range(1, BANK_F // P))
+                    multiply_by_tile(n, range(BANK_F // P))
                 statistics(n)
                 inverse_deviation(n)
             if n >= 2:
@@ -306,3 +295,7 @@ def tile_graphconvolutionbatch_w_kernel(tc, H, W_words, W_scales, gamma, beta, o
                 store(n - 2)
             if n < n_banks:
                 gain_and_shift(n)
+            if 1 <= n <= n_banks:
+                to_rows(n - 1)
+                split_high(n - 1)
+                split_low(n - 1)

@@ -20,8 +20,10 @@ PACK = 4
 K_PASS = P * PACK
 PASSES = K // K_PASS
 PLANES_PER_TILE = 4
-BANK_F = 512
-LAST_F = 256
+PSUM_F = 512
+LOAD_F = 512
+BANK_F = 256
+TILES = BANK_F // P
 N_TILES = FEATURES // P
 EPS_BN = 1e-5
 EPS_DEG = 1e-5
@@ -36,8 +38,8 @@ def tile_graphconvolutionbatch_w_kernel(tc, H, W_words, W_scales, gamma, beta, o
     w_words = W_words.rearrange("g p n t -> g p (n t)").bitcast(I32).rearrange("g p n -> p g n")
     w_scale_rows = W_scales.bitcast(F32)
 
-    range_widths = [BANK_F] * (FEATURES // BANK_F - 1) + [LAST_F] * (BANK_F // LAST_F)
-    range_pieces = [[2, 2, 2, 2]] * (FEATURES // BANK_F - 1) + [[4, 4], [4, 3, 1]]
+    range_widths = [LOAD_F] * (FEATURES // LOAD_F - 1) + [BANK_F] * (LOAD_F // BANK_F)
+    range_pieces = [[2, 2, 2, 2]] * (FEATURES // LOAD_F - 1) + [[4, 4], [4, 3, 1]]
 
     with ExitStack() as ctx:
         ctx.enter_context(tc.manual_schedule())
@@ -65,7 +67,9 @@ def tile_graphconvolutionbatch_w_kernel(tc, H, W_words, W_scales, gamma, beta, o
                 piece = weights.tile([P, passes, width], U32, name="w_%d_%d" % (first, g), align_bytes=64)
                 nc.sync.dma_start(out=piece[:].bitcast(I32), in_=w_words[:, g : g + passes, first : first + width])
                 words.extend([piece[:, j, :] for j in range(passes)])
-            banks.append((words, pieces[0], first, width))
+            result = results.tile([P, width], F32, name="result_%d" % first)
+            for column in range(0, width, BANK_F):
+                banks.append((words, column, first + column, result, width))
             first += width
         n_banks = len(banks)
 
@@ -162,11 +166,11 @@ def tile_graphconvolutionbatch_w_kernel(tc, H, W_words, W_scales, gamma, beta, o
         summed = {}
 
         def one_pass(n, i, g):
-            words, first_f = banks[n][0], banks[n][2]
+            words, column, first_f = banks[n][0], banks[n][1], banks[n][2]
             offset = 4 * (g % PLANES_PER_TILE)
             nc.tensor.matmul_mx(
                 out=acc[n][i],
-                lhsT=words[g][:, P * i : P * (i + 1)].bitcast(FP8X4),
+                lhsT=words[g][:, column + P * i : column + P * (i + 1)].bitcast(FP8X4),
                 lhsT_scale=w_planes[offset:P, g // PLANES_PER_TILE, first_f + P * i : first_f + P * (i + 1)],
                 rhs=h_codes[:, g, :].bitcast(FP8X4),
                 rhs_scale=h_scales[:, g, :],
@@ -174,64 +178,43 @@ def tile_graphconvolutionbatch_w_kernel(tc, H, W_words, W_scales, gamma, beta, o
                 stop=(g == PASSES - 1),
             )
 
-        def multiply_by_tile(n, tiles):
-            if n not in acc:
-                bank = psum.tile([P, BANK_F // P, P], F32, name="acc", bufs=4)
-                acc[n] = [bank[:, i, :] for i in range(BANK_F // P)]
-            for i in tiles:
-                for g in range(PASSES):
-                    one_pass(n, i, g)
-
-        def multiply_by_pass(n, passes):
-            if n not in acc:
-                acc[n] = []
-                for i in range(banks[n][3] // P):
-                    bank = psum.tile([P, BANK_F // P, P], F32, name="acc", bufs=4)
-                    acc[n].append(bank[:, 0, :])
-            for g in passes:
-                for i in range(banks[n][3] // P):
+        def multiply(n):
+            acc[n] = []
+            for i in range(TILES):
+                bank = psum.tile([P, PSUM_F // P, P], F32, name="acc", bufs=4)
+                acc[n].append(bank[:, 0, :])
+            for g in range(PASSES):
+                for i in range(TILES):
                     one_pass(n, i, g)
 
         def statistics(n):
-            first_f, bank_f = banks[n][2], banks[n][3]
-            tiles = bank_f // P
-            t0 = first_f // P
-            stats = small.tile([P, BANK_F // P, 6], F32)
-            mean_var[n] = small.tile([P, BANK_F // P, 2], F32, name="mean_var")
-            for i in range(tiles):
+            t0 = banks[n][2] // P
+            stats = small.tile([P, TILES, 6], F32)
+            mean_var[n] = small.tile([P, TILES, 2], F32, name="mean_var")
+            for i in range(TILES):
                 nc.vector.bn_stats(out=stats[:, i, :], in_=acc[n][i])
-            for i in range(tiles):
+            for i in range(TILES):
                 nc.vector.bn_aggr(out=mean_var[n][:, i, :], in_=stats[:, i, :])
-            mean_gamma[n] = small.tile([P, BANK_F // P], F32, name="mean_gamma")
-            nc.vector.tensor_mul(
-                out=mean_gamma[n][:, 0:tiles], in0=mean_var[n][:, 0:tiles, 0], in1=gb[:, t0 : t0 + tiles]
-            )
+            mean_gamma[n] = small.tile([P, TILES], F32, name="mean_gamma")
+            nc.vector.tensor_mul(out=mean_gamma[n][:], in0=mean_var[n][:, :, 0], in1=gb[:, t0 : t0 + TILES])
 
         def inverse_deviation(n):
-            tiles = banks[n][3] // P
-            inv_std[n] = small.tile([P, BANK_F // P], F32, name="inv_std")
+            inv_std[n] = small.tile([P, TILES], F32, name="inv_std")
             nc.scalar.activation(
-                out=inv_std[n][:, 0:tiles],
-                in_=mean_var[n][:, 0:tiles, 1],
-                func=ACT.Abs_reciprocal_sqrt,
-                bias=eps_bn[:, 0:1],
+                out=inv_std[n][:], in_=mean_var[n][:, :, 1], func=ACT.Abs_reciprocal_sqrt, bias=eps_bn[:, 0:1]
             )
 
         def gain_and_shift(n):
-            first_f, bank_f = banks[n][2], banks[n][3]
-            tiles = bank_f // P
-            t0 = first_f // P
-            shift[n] = small.tile([P, BANK_F // P], F32, name="shift")
-            nc.vector.tensor_mul(out=shift[n][:, 0:tiles], in0=mean_gamma[n][:, 0:tiles], in1=inv_std[n][:, 0:tiles])
-            gain[n] = small.tile([P, BANK_F // P], F32, name="gain")
-            nc.vector.tensor_mul(out=gain[n][:, 0:tiles], in0=inv_std[n][:, 0:tiles], in1=gb[:, t0 : t0 + tiles])
-            nc.vector.tensor_sub(
-                out=shift[n][:, 0:tiles], in0=gb[:, N_TILES + t0 : N_TILES + t0 + tiles], in1=shift[n][:, 0:tiles]
-            )
+            t0 = banks[n][2] // P
+            shift[n] = small.tile([P, TILES], F32, name="shift")
+            nc.vector.tensor_mul(out=shift[n][:], in0=mean_gamma[n][:], in1=inv_std[n][:])
+            gain[n] = small.tile([P, TILES], F32, name="gain")
+            nc.vector.tensor_mul(out=gain[n][:], in0=inv_std[n][:], in1=gb[:, t0 : t0 + TILES])
+            nc.vector.tensor_sub(out=shift[n][:], in0=gb[:, N_TILES + t0 : N_TILES + t0 + TILES], in1=shift[n][:])
 
         def norm_and_relu(n):
-            z_feat[n] = work.tile([P, BANK_F // P, P], F32, name="z_feat")
-            for i in range(banks[n][3] // P):
+            z_feat[n] = work.tile([P, TILES, P], F32, name="z_feat")
+            for i in range(TILES):
                 nc.scalar.activation(
                     out=z_feat[n][:, i, :],
                     in_=acc[n][i],
@@ -242,52 +225,35 @@ def tile_graphconvolutionbatch_w_kernel(tc, H, W_words, W_scales, gamma, beta, o
 
         def to_rows(n):
             z_psum[n] = psum.tile([P, BANK_F], F32, name="z_psum")
-            for i in range(banks[n][3] // P):
+            for i in range(TILES):
                 nc.tensor.transpose(z_psum[n][:, P * i : P * (i + 1)], z_feat[n][:, i, :], ident[:])
 
         def split_high(n):
-            bank_f = banks[n][3]
             z_high[n] = work.tile([P, BANK_F], BF16, name="z_high")
-            nc.scalar.activation(
-                out=z_high[n][:, 0:bank_f], in_=z_psum[n][:, 0:bank_f], func=ACT.Copy, scale=d[:, 0:1]
-            )
+            nc.scalar.activation(out=z_high[n][:], in_=z_psum[n][:], func=ACT.Copy, scale=d[:, 0:1])
 
         def split_low(n):
-            bank_f = banks[n][3]
             z_low[n] = work.tile([P, BANK_F], BF16, name="z_low")
             nc.vector.scalar_tensor_tensor(
-                out=z_low[n][:, 0:bank_f],
-                in0=z_psum[n][:, 0:bank_f],
-                scalar=d[:, 0:1],
-                in1=z_high[n][:, 0:bank_f],
-                op0=ALU.mult,
-                op1=ALU.subtract,
+                out=z_low[n][:], in0=z_psum[n][:], scalar=d[:, 0:1], in1=z_high[n][:], op0=ALU.mult, op1=ALU.subtract
             )
 
         def aggregate(n):
-            bank_f = banks[n][3]
             summed[n] = psum.tile([P, BANK_F], F32, name="summed")
-            nc.tensor.matmul(
-                out=summed[n][:, 0:bank_f], lhsT=neighbours_bf[:], rhs=z_high[n][:, 0:bank_f], start=True, stop=False
-            )
-            nc.tensor.matmul(
-                out=summed[n][:, 0:bank_f], lhsT=neighbours_bf[:], rhs=z_low[n][:, 0:bank_f], start=False, stop=True
-            )
+            nc.tensor.matmul(out=summed[n][:], lhsT=neighbours_bf[:], rhs=z_high[n][:], start=True, stop=False)
+            nc.tensor.matmul(out=summed[n][:], lhsT=neighbours_bf[:], rhs=z_low[n][:], start=False, stop=True)
 
         def store(n):
-            first_f, bank_f = banks[n][2], banks[n][3]
-            result = results.tile([P, bank_f], F32, name="result_%d" % n)
-            nc.vector.tensor_scalar_mul(out=result[:], in0=summed[n][:, 0:bank_f], scalar1=d[:, 0:1])
-            nc.sync.dma_start(out=out_rows[:, first_f : first_f + bank_f], in_=result[:])
+            column, first_f, result, width = banks[n][1], banks[n][2], banks[n][3], banks[n][4]
+            nc.vector.tensor_scalar_mul(out=result[:, column : column + BANK_F], in0=summed[n][:], scalar1=d[:, 0:1])
+            if column + BANK_F == width:
+                nc.sync.dma_start(out=out_rows[:, first_f + BANK_F - width : first_f + BANK_F], in_=result[:])
 
         for n in range(n_banks + 2):
             if 1 <= n <= n_banks:
                 norm_and_relu(n - 1)
             if n < n_banks:
-                if banks[n][3] < BANK_F:
-                    multiply_by_pass(n, range(PASSES))
-                else:
-                    multiply_by_tile(n, range(BANK_F // P))
+                multiply(n)
                 statistics(n)
                 inverse_deviation(n)
             if n >= 2:

@@ -223,33 +223,54 @@ def tile_graphconvolutionbatch_w_kernel(tc, H, W_words, W_scales, gamma, beta, o
                     bias=shift[n][:, i : i + 1],
                 )
 
-        def to_rows(n):
-            z_psum[n] = psum.tile([P, BANK_F], F32, name="z_psum")
-            for i in range(TILES):
-                nc.tensor.transpose(z_psum[n][:, P * i : P * (i + 1)], z_feat[n][:, i, :], ident[:])
+        def columns(tiles):
+            return slice(P * tiles[0], P * (tiles[-1] + 1))
 
-        def split_high(n):
-            z_high[n] = work.tile([P, BANK_F], BF16, name="z_high")
-            nc.scalar.activation(out=z_high[n][:], in_=z_psum[n][:], func=ACT.Copy, scale=d[:, 0:1])
+        def to_rows(n, tiles):
+            bank = psum.tile([P, BANK_F], F32, name="z_psum")
+            for i in tiles:
+                nc.tensor.transpose(bank[:, P * i : P * (i + 1)], z_feat[n][:, i, :], ident[:])
+                z_psum[n, i] = bank
 
-        def split_low(n):
-            z_low[n] = work.tile([P, BANK_F], BF16, name="z_low")
+        def split_high(n, tiles):
+            cols = columns(tiles)
+            if n not in z_high:
+                z_high[n] = work.tile([P, BANK_F], BF16, name="z_high")
+            nc.scalar.activation(out=z_high[n][:, cols], in_=z_psum[n, tiles[0]][:, cols], func=ACT.Copy, scale=d[:, 0:1])
+
+        def split_low(n, tiles):
+            cols = columns(tiles)
+            if n not in z_low:
+                z_low[n] = work.tile([P, BANK_F], BF16, name="z_low")
             nc.vector.scalar_tensor_tensor(
-                out=z_low[n][:], in0=z_psum[n][:], scalar=d[:, 0:1], in1=z_high[n][:], op0=ALU.mult, op1=ALU.subtract
+                out=z_low[n][:, cols],
+                in0=z_psum[n, tiles[0]][:, cols],
+                scalar=d[:, 0:1],
+                in1=z_high[n][:, cols],
+                op0=ALU.mult,
+                op1=ALU.subtract,
             )
 
-        def aggregate(n):
-            summed[n] = psum.tile([P, BANK_F], F32, name="summed")
-            nc.tensor.matmul(out=summed[n][:], lhsT=neighbours_bf[:], rhs=z_high[n][:], start=True, stop=False)
-            nc.tensor.matmul(out=summed[n][:], lhsT=neighbours_bf[:], rhs=z_low[n][:], start=False, stop=True)
+        def aggregate(n, tiles):
+            cols = columns(tiles)
+            bank = psum.tile([P, BANK_F], F32, name="summed")
+            nc.tensor.matmul(out=bank[:, cols], lhsT=neighbours_bf[:], rhs=z_high[n][:, cols], start=True, stop=False)
+            nc.tensor.matmul(out=bank[:, cols], lhsT=neighbours_bf[:], rhs=z_low[n][:, cols], start=False, stop=True)
+            summed[n, tiles[0]] = bank
 
-        def store(n):
+        def store(n, tiles):
             column, first_f, result, width = banks[n][1], banks[n][2], banks[n][3], banks[n][4]
-            nc.vector.tensor_scalar_mul(out=result[:, column : column + BANK_F], in0=summed[n][:], scalar1=d[:, 0:1])
-            if column + BANK_F == width:
+            cols = columns(tiles)
+            nc.vector.tensor_scalar_mul(
+                out=result[:, column + cols.start : column + cols.stop], in0=summed[n, tiles[0]][:, cols], scalar1=d[:, 0:1]
+            )
+            if column + cols.stop == width:
                 nc.sync.dma_start(out=out_rows[:, first_f + BANK_F - width : first_f + BANK_F], in_=result[:])
 
-        for n in range(n_banks + 2):
+        whole = [list(range(TILES))]
+        by_tile = [[i] for i in range(TILES)]
+        last = n_banks - 1
+        for n in range(n_banks + 1):
             if 1 <= n <= n_banks:
                 norm_and_relu(n - 1)
             if n < n_banks:
@@ -257,11 +278,12 @@ def tile_graphconvolutionbatch_w_kernel(tc, H, W_words, W_scales, gamma, beta, o
                 statistics(n)
                 inverse_deviation(n)
             if n >= 2:
-                aggregate(n - 2)
-                store(n - 2)
+                aggregate(n - 2, whole[0])
+                store(n - 2, whole[0])
             if n < n_banks:
                 gain_and_shift(n)
             if 1 <= n <= n_banks:
-                to_rows(n - 1)
-                split_high(n - 1)
-                split_low(n - 1)
+                parts = by_tile if n - 1 == last else whole
+                for step in [to_rows, split_high, split_low] + ([aggregate, store] if n - 1 == last else []):
+                    for tiles in parts:
+                        step(n - 1, tiles)

@@ -196,7 +196,14 @@ def tile_graphconvolutionbatch_w_kernel(tc, H, W_words, W_scales, gamma, beta, o
             for i in range(TILES):
                 nc.vector.bn_aggr(out=mean_var[n][:, i, :], in_=stats[:, i, :])
             mean_gamma[n] = small.tile([P, TILES], F32, name="mean_gamma")
-            nc.vector.tensor_mul(out=mean_gamma[n][:], in0=mean_var[n][:, :, 0], in1=gb[:, t0 : t0 + TILES])
+            nc.vector.scalar_tensor_tensor(
+                out=mean_gamma[n][:],
+                in0=mean_var[n][:, :, 0],
+                scalar=-1.0,
+                in1=gb[:, t0 : t0 + TILES],
+                op0=ALU.mult,
+                op1=ALU.mult,
+            )
 
         def inverse_deviation(n):
             inv_std[n] = small.tile([P, TILES], F32, name="inv_std")
@@ -207,10 +214,19 @@ def tile_graphconvolutionbatch_w_kernel(tc, H, W_words, W_scales, gamma, beta, o
         def gain_and_shift(n):
             t0 = banks[n][2] // P
             shift[n] = small.tile([P, TILES], F32, name="shift")
-            nc.vector.tensor_mul(out=shift[n][:], in0=mean_gamma[n][:], in1=inv_std[n][:])
             gain[n] = small.tile([P, TILES], F32, name="gain")
-            nc.vector.tensor_mul(out=gain[n][:], in0=inv_std[n][:], in1=gb[:, t0 : t0 + TILES])
-            nc.vector.tensor_sub(out=shift[n][:], in0=gb[:, N_TILES + t0 : N_TILES + t0 + TILES], in1=shift[n][:])
+            for i in range(TILES):
+                one = slice(i, i + 1)
+                nc.scalar.activation(
+                    out=gain[n][:, one], in_=gb[:, t0 + i : t0 + i + 1], func=ACT.Copy, scale=inv_std[n][:, one]
+                )
+                nc.scalar.activation(
+                    out=shift[n][:, one],
+                    in_=mean_gamma[n][:, one],
+                    func=ACT.Identity,
+                    scale=inv_std[n][:, one],
+                    bias=gb[:, N_TILES + t0 + i : N_TILES + t0 + i + 1],
+                )
 
         def norm_and_relu(n):
             z_feat[n] = work.tile([P, TILES, P], F32, name="z_feat")
@@ -272,6 +288,7 @@ def tile_graphconvolutionbatch_w_kernel(tc, H, W_words, W_scales, gamma, beta, o
         last = n_banks - 1
         for n in range(n_banks + 1):
             if 1 <= n <= n_banks:
+                gain_and_shift(n - 1)
                 norm_and_relu(n - 1)
             if n < n_banks:
                 multiply(n)
@@ -280,8 +297,6 @@ def tile_graphconvolutionbatch_w_kernel(tc, H, W_words, W_scales, gamma, beta, o
             if n >= 2:
                 aggregate(n - 2, whole[0])
                 store(n - 2, whole[0])
-            if n < n_banks:
-                gain_and_shift(n)
             if 1 <= n <= n_banks:
                 parts = by_tile if n - 1 == last else whole
                 for step in [to_rows, split_high, split_low] + ([aggregate, store] if n - 1 == last else []):

from contextlib import ExitStack

import concourse.mybir as mybir
from concourse.masks import make_identity

F32 = mybir.dt.float32
BF16 = mybir.dt.bfloat16
I32 = mybir.dt.int32
U32 = mybir.dt.uint32
U8 = mybir.dt.uint8
FP8X4 = mybir.dt.float8_e4m3fn_x4
ACT = mybir.ActivationFunctionType
ALU = mybir.AluOpType

P = 128
BATCH, GRID = 2, 8
K = 4096
FEATURES = 4096
PACK = 4
K_PASS = P * PACK
PASSES = K // K_PASS
PLANES_PER_TILE = 4
PSUM_F = 512
LOAD_F = 512
BANK_F = 256
TILES = BANK_F // P
N_TILES = FEATURES // P
EPS_BN = 1e-5
EPS_DEG = 1e-5

FLOPS = 2 * P * K * FEATURES


def tile_graphconvolutionbatch_w_kernel(tc, H, W_words, W_scales, gamma, beta, out):
    nc = tc.nc
    h_rows = H.rearrange("b n k -> (b n) k")
    out_rows = out.rearrange("b n f -> (b n) f")
    w_words = W_words.rearrange("g p n t -> g p (n t)").bitcast(I32).rearrange("g p n -> p g n")
    w_scale_rows = W_scales.bitcast(F32)

    range_widths = [LOAD_F] * (FEATURES // LOAD_F - 1) + [BANK_F] * (LOAD_F // BANK_F)
    range_pieces = [[2, 2, 2, 2]] * (FEATURES // LOAD_F - 1) + [[4, 4], [4, 3, 1]]

    with ExitStack() as ctx:
        ctx.enter_context(tc.manual_schedule())
        consts = ctx.enter_context(tc.tile_pool(name="consts", bufs=1))
        weights = ctx.enter_context(tc.tile_pool(name="weights", bufs=1))
        results = ctx.enter_context(tc.tile_pool(name="results", bufs=1))
        small = ctx.enter_context(tc.tile_pool(name="small", bufs=4))
        work = ctx.enter_context(tc.tile_pool(name="work", bufs=3))

        w_planes = consts.tile([P, PASSES // PLANES_PER_TILE, FEATURES], U8, align_bytes=64)
        nc.vector.memset(w_planes[:].bitcast(I32), 0)

        h_sb = []
        for pair in range(PASSES // 2):
            h_piece = consts.tile([P, 2 * K_PASS], BF16, name="h_sb_%d" % pair)
            nc.sync.dma_start(out=h_piece[:], in_=h_rows[:, 2 * K_PASS * pair : 2 * K_PASS * (pair + 1)])
            h_sb.append(h_piece)

        banks = []
        first = 0
        for width, pieces in zip(range_widths, range_pieces):
            words = []
            for passes in pieces:
                g = len(words)
                piece = weights.tile([P, passes, width], U32, name="w_%d_%d" % (first, g), align_bytes=64)
                nc.sync.dma_start(out=piece[:].bitcast(I32), in_=w_words[:, g : g + passes, first : first + width])
                words.extend([piece[:, j, :] for j in range(passes)])
            result = results.tile([P, width], F32, name="result_%d" % first)
            for column in range(0, width, BANK_F):
                banks.append((words, column, first + column, result, width))
            first += width
        n_banks = len(banks)

        gb_rows = consts.tile([P, P], BF16)
        nc.vector.memset(gb_rows[:], 0.0)
        nc.scalar.dma_start(out=gb_rows[0:N_TILES, :], in_=gamma.rearrange("(t f) -> t f", f=P))
        nc.scalar.dma_start(out=gb_rows[N_TILES : 2 * N_TILES, :], in_=beta.rearrange("(t f) -> t f", f=P))

        ident = consts.tile([P, P], F32)
        make_identity(nc, ident[:])

        for group in range(PASSES // PLANES_PER_TILE):
            for quad in (0, 2, 1, 3):
                nc.gpsimd.dma_start(
                    out=w_planes[32 * quad : 32 * quad + 16, group, :].bitcast(F32),
                    in_=w_scale_rows[4 * group : 4 * group + 4, 4 * quad : 4 * quad + 4, :],
                )
        eps_bn = consts.tile([P, 1], F32)
        nc.vector.memset(eps_bn[:], EPS_BN)
        eps_deg = consts.tile([P, 1], F32)
        nc.vector.memset(eps_deg[:], EPS_DEG)

        ident_c = ident[:].rearrange("p (s c) -> p s c", c=GRID)
        along_c = consts.tile([P, BATCH * GRID, GRID], F32)
        nc.vector.tensor_copy(out=along_c[:], in_=ident_c)
        nc.vector.tensor_add(out=along_c[:, :, 1:GRID], in0=along_c[:, :, 1:GRID], in1=ident_c[:, :, 0 : GRID - 1])
        nc.vector.tensor_add(out=along_c[:, :, 0 : GRID - 1], in0=along_c[:, :, 0 : GRID - 1], in1=ident_c[:, :, 1:GRID])
        along_c_r = along_c[:].rearrange("p (b r) c -> p b (r c)", b=BATCH)
        neighbours = consts.tile([P, BATCH, GRID * GRID], F32)
        nc.vector.tensor_copy(out=neighbours[:], in_=along_c_r)
        inner = GRID * (GRID - 1)
        nc.vector.tensor_add(out=neighbours[:, :, GRID:], in0=neighbours[:, :, GRID:], in1=along_c_r[:, :, 0:inner])
        nc.vector.tensor_add(out=neighbours[:, :, 0:inner], in0=neighbours[:, :, 0:inner], in1=along_c_r[:, :, GRID:])
        neighbours_2d = neighbours[:].rearrange("p b s -> p (b s)")

        degree = consts.tile([P, 1], F32)
        nc.vector.reduce_sum(out=degree[:], in_=neighbours_2d, axis=mybir.AxisListType.X)
        d = consts.tile([P, 1], F32)
        nc.scalar.activation(out=d[:], in_=degree[:], func=ACT.Abs_reciprocal_sqrt, bias=eps_deg[:, 0:1])

        grouped = consts.tile([P, PASSES, P, PACK], BF16, align_bytes=64)
        h_codes = consts.tile([P, PASSES, P], U32, align_bytes=64)
        h_scales = consts.tile([P, PASSES, P], U8, align_bytes=64)
        gb = consts.tile([P, 2 * N_TILES], F32)
        neighbours_bf = consts.tile([P, P], BF16)
        nc.vector.tensor_copy(out=neighbours_bf[:], in_=neighbours_2d)
        with tc.psum_pool(name="head_psum", bufs=1) as head_psum:
            grouped_pairs = grouped[:].bitcast(F32)

            def quantise(pair):
                gs = slice(2 * pair, 2 * pair + 2)
                nc.vector.quantize_mx(
                    out=h_codes[:, gs, :].rearrange("p g r -> p (g r)").bitcast(FP8X4),
                    scales=h_scales[:, gs, :].rearrange("p g r -> p (g r)"),
                    in_=grouped[:, gs, :, :].rearrange("p g r t -> p (g r t)"),
                )

            for pair in range(PASSES // 2):
                flipped = head_psum.tile([P, 2, 2, P], F32, name="flipped_%d" % pair)
                h_pairs = h_sb[pair][:].bitcast(F32)
                for gg in range(2):
                    for u in range(2):
                        nc.tensor.transpose(
                            flipped[:, gg, u, :], h_pairs[:, 256 * gg + u : 256 * (gg + 1) : 2], ident[:]
                        )
                dst = grouped_pairs[:, 2 * pair : 2 * pair + 2, :, :]
                src = flipped[:].rearrange("p g u r -> p g r u")
                if pair % 2 == 0:
                    nc.vector.tensor_copy(out=dst, in_=src)
                else:
                    nc.scalar.copy(out=dst, in_=src)
                if pair >= 1:
                    quantise(pair - 1)
            quantise(PASSES // 2 - 1)

            gb_rows_f32 = consts.tile([P, P], F32)
            nc.vector.tensor_copy(out=gb_rows_f32[:], in_=gb_rows[:])
            gb_flipped = head_psum.tile([P, P], F32)
            nc.tensor.transpose(gb_flipped[:], gb_rows_f32[:], ident[:])
            nc.vector.tensor_copy(out=gb[:], in_=gb_flipped[:, 0 : 2 * N_TILES])


        psum = ctx.enter_context(tc.psum_pool(name="psum", bufs=2))
        acc = {}
        mean_var = {}
        mean_gamma = {}
        inv_std = {}
        gain = {}
        shift = {}
        z_feat = {}
        z_psum = {}
        z_high = {}
        z_low = {}
        summed = {}

        def one_pass(n, i, g):
            words, column, first_f = banks[n][0], banks[n][1], banks[n][2]
            offset = 4 * (g % PLANES_PER_TILE)
            nc.tensor.matmul_mx(
                out=acc[n][i],
                lhsT=words[g][:, column + P * i : column + P * (i + 1)].bitcast(FP8X4),
                lhsT_scale=w_planes[offset:P, g // PLANES_PER_TILE, first_f + P * i : first_f + P * (i + 1)],
                rhs=h_codes[:, g, :].bitcast(FP8X4),
                rhs_scale=h_scales[:, g, :],
                start=(g == 0),
                stop=(g == PASSES - 1),
            )

        def multiply(n):
            acc[n] = []
            for i in range(TILES):
                bank = psum.tile([P, PSUM_F // P, P], F32, name="acc", bufs=4)
                acc[n].append(bank[:, 0, :])
            for g in range(PASSES):
                for i in range(TILES):
                    one_pass(n, i, g)

        def statistics(n):
            t0 = banks[n][2] // P
            stats = small.tile([P, TILES, 6], F32)
            mean_var[n] = small.tile([P, TILES, 2], F32, name="mean_var")
            for i in range(TILES):
                nc.vector.bn_stats(out=stats[:, i, :], in_=acc[n][i])
            for i in range(TILES):
                nc.vector.bn_aggr(out=mean_var[n][:, i, :], in_=stats[:, i, :])
            mean_gamma[n] = small.tile([P, TILES], F32, name="mean_gamma")
            nc.vector.scalar_tensor_tensor(
                out=mean_gamma[n][:],
                in0=mean_var[n][:, :, 0],
                scalar=-1.0,
                in1=gb[:, t0 : t0 + TILES],
                op0=ALU.mult,
                op1=ALU.mult,
            )

        def inverse_deviation(n):
            inv_std[n] = small.tile([P, TILES], F32, name="inv_std")
            nc.scalar.activation(
                out=inv_std[n][:], in_=mean_var[n][:, :, 1], func=ACT.Abs_reciprocal_sqrt, bias=eps_bn[:, 0:1]
            )

        def gain_and_shift(n):
            t0 = banks[n][2] // P
            shift[n] = small.tile([P, TILES], F32, name="shift")
            gain[n] = small.tile([P, TILES], F32, name="gain")
            for i in range(TILES):
                one = slice(i, i + 1)
                nc.scalar.activation(
                    out=gain[n][:, one], in_=gb[:, t0 + i : t0 + i + 1], func=ACT.Copy, scale=inv_std[n][:, one]
                )
                nc.scalar.activation(
                    out=shift[n][:, one],
                    in_=mean_gamma[n][:, one],
                    func=ACT.Identity,
                    scale=inv_std[n][:, one],
                    bias=gb[:, N_TILES + t0 + i : N_TILES + t0 + i + 1],
                )

        def norm_and_relu(n):
            z_feat[n] = work.tile([P, TILES, P], F32, name="z_feat")
            for i in range(TILES):
                nc.scalar.activation(
                    out=z_feat[n][:, i, :],
                    in_=acc[n][i],
                    func=ACT.Relu,
                    scale=gain[n][:, i : i + 1],
                    bias=shift[n][:, i : i + 1],
                )

        def columns(tiles):
            return slice(P * tiles[0], P * (tiles[-1] + 1))

        def to_rows(n, tiles):
            bank = psum.tile([P, BANK_F], F32, name="z_psum")
            for i in tiles:
                nc.tensor.transpose(bank[:, P * i : P * (i + 1)], z_feat[n][:, i, :], ident[:])
                z_psum[n, i] = bank

        def split_high(n, tiles):
            cols = columns(tiles)
            if n not in z_high:
                z_high[n] = work.tile([P, BANK_F], BF16, name="z_high")
            nc.scalar.activation(out=z_high[n][:, cols], in_=z_psum[n, tiles[0]][:, cols], func=ACT.Copy, scale=d[:, 0:1])

        def split_low(n, tiles):
            cols = columns(tiles)
            if n not in z_low:
                z_low[n] = work.tile([P, BANK_F], BF16, name="z_low")
            nc.vector.scalar_tensor_tensor(
                out=z_low[n][:, cols],
                in0=z_psum[n, tiles[0]][:, cols],
                scalar=d[:, 0:1],
                in1=z_high[n][:, cols],
                op0=ALU.mult,
                op1=ALU.subtract,
            )

        def aggregate(n, tiles):
            cols = columns(tiles)
            bank = psum.tile([P, BANK_F], F32, name="summed")
            nc.tensor.matmul(out=bank[:, cols], lhsT=neighbours_bf[:], rhs=z_high[n][:, cols], start=True, stop=False)
            nc.tensor.matmul(out=bank[:, cols], lhsT=neighbours_bf[:], rhs=z_low[n][:, cols], start=False, stop=True)
            summed[n, tiles[0]] = bank

        def store(n, tiles):
            column, first_f, result, width = banks[n][1], banks[n][2], banks[n][3], banks[n][4]
            cols = columns(tiles)
            nc.vector.tensor_scalar_mul(
                out=result[:, column + cols.start : column + cols.stop], in0=summed[n, tiles[0]][:, cols], scalar1=d[:, 0:1]
            )
            if column + cols.stop == width:
                nc.sync.dma_start(out=out_rows[:, first_f + BANK_F - width : first_f + BANK_F], in_=result[:])

        whole = [list(range(TILES))]
        by_tile = [[i] for i in range(TILES)]
        last = n_banks - 1
        for n in range(n_banks + 1):
            if 1 <= n <= n_banks:
                gain_and_shift(n - 1)
                norm_and_relu(n - 1)
            if n < n_banks:
                multiply(n)
                statistics(n)
                inverse_deviation(n)
            if n >= 2:
                aggregate(n - 2, whole[0])
                store(n - 2, whole[0])
            if 1 <= n <= n_banks:
                parts = by_tile if n - 1 == last else whole
                for step in [to_rows, split_high, split_low] + ([aggregate, store] if n - 1 == last else []):
                    for tiles in parts:
                        step(n - 1, tiles)
